import numpy as np
import ml_dtypes


def mxq(x, axis, fmt="e4m3"):
    dtype, down = {"e4m3": (ml_dtypes.float8_e4m3fn, 7), "e5m2": (ml_dtypes.float8_e5m2, 14)}[fmt]
    v = np.moveaxis(np.asarray(x, np.float32).astype(ml_dtypes.bfloat16).astype(np.float64), axis, -1)
    blocks = v.reshape(v.shape[:-1] + (-1, 32))
    amax = np.abs(blocks).max(-1, keepdims=True)
    byte = np.maximum(np.where(amax > 0, np.frexp(amax)[1] - 1 + 127, 0) - down, 1)
    scale = np.exp2(byte - 127.0)
    codes = (blocks / scale).astype(np.float32).astype(dtype).astype(np.float64)
    return np.moveaxis((codes * scale).reshape(v.shape), -1, axis)


WIDE = False


def mx_kscale(k):
    if not WIDE:
        return np.ones(k)
    levels = np.array([10, -10, 5, -5, 0])
    a = np.random.permutation(np.resize(levels, k // 512 * 4)).reshape(k // 512, 4)
    idx = np.arange(k)
    return np.exp2(a[idx // 512, idx % 128 // 32])


BF16 = ml_dtypes.bfloat16


def bf(x):
    return np.asarray(x, np.float32).astype(BF16)


def f64(x):
    return np.asarray(x).astype(np.float64)


E2M1 = np.array([0.0, 0.5, 1.0, 1.5, 2.0, 3.0, 4.0, 6.0, -0.0, -0.5, -1.0, -1.5, -2.0, -3.0, -4.0, -6.0])


def pack_weight(w, fmt):
    k, n = w.shape
    w = f64(bf(w)).reshape(k // 32, 32, n)
    amax = np.abs(w).max(1)
    if fmt == "e4m3":
        byte = np.frexp(amax)[1] - 1 + 127 - 7
    else:
        mant, ex = np.frexp(amax / 6.0)
        byte = np.where(mant > 0.5, ex, ex - 1) + 127
    byte = np.clip(np.where(amax > 0, byte, 1), 1, 254)
    scaled = (w * np.exp2(127.0 - byte)[:, None, :]).reshape(k, n).astype(np.float32)
    by_word = np.ascontiguousarray(scaled.reshape(k // 512, 128, 4, n).transpose(0, 1, 3, 2))
    if fmt == "e4m3":
        words = by_word.astype(ml_dtypes.float8_e4m3fn).view(np.uint8)
    else:
        c = by_word.astype(ml_dtypes.float4_e2m1fn).view(np.uint8) & 0xF
        words = c[..., 0::2] | (c[..., 1::2] << 4)
    return np.ascontiguousarray(words), np.ascontiguousarray(byte.astype(np.uint8).reshape(k // 512, 16, n))


def unpack_weight(words, scales, fmt):
    g, p, n, _ = words.shape
    if fmt == "e4m3":
        vals = np.ascontiguousarray(words).view(ml_dtypes.float8_e4m3fn).astype(np.float64)
    else:
        nib = np.empty((g, p, n, 4), np.uint8)
        nib[..., 0::2] = words & 0xF
        nib[..., 1::2] = words >> 4
        vals = E2M1[nib]
    vals = vals * np.repeat(np.exp2(scales.astype(np.float64) - 127.0), 8, axis=1)[..., None]
    return vals.transpose(0, 1, 3, 2).reshape(g * 512, n)


B, IDIM, HDIM, ODIM, S, DEPTH, NACT, NTOP = 4096, 512, 1024, 512, 128, 4, 3, 2
FMT = "e4m3"


def sigmoid(v):
    return 1.0 / (1.0 + np.exp(-v))


def setup_inputs():
    s = mx_kscale(HDIM)
    h = bf(sigmoid(np.random.standard_normal((B, HDIM)) * 1.3) * s)
    stack = bf(np.random.standard_normal((B, DEPTH, S)))
    Wa_words, Wa_scales = pack_weight((np.random.standard_normal((NACT * S, HDIM)) * 3.0 / np.sqrt(HDIM) / s).T, FMT)
    ba = bf(np.random.standard_normal(NACT * S) * 0.5)
    Ws_words, Ws_scales = pack_weight((np.random.standard_normal((S, HDIM)) * 2.0 / np.sqrt(HDIM) / s).T, FMT)
    bs = bf(np.random.standard_normal(S))
    Wo_words, Wo_scales = pack_weight((np.random.standard_normal((ODIM, HDIM)) * 2.0 / np.sqrt(HDIM) / s).T, FMT)
    bo = bf(np.random.standard_normal(ODIM) * 0.3)
    return {"h": h,
            "stack": stack,
            "Wa_words": Wa_words,
            "Wa_scales": Wa_scales,
            "ba": ba,
            "Ws_words": Ws_words,
            "Ws_scales": Ws_scales,
            "bs": bs,
            "Wo_words": Wo_words,
            "Wo_scales": Wo_scales,
            "bo": bo}


def reference(h, stack, Wa_words, Wa_scales, ba, Ws_words, Ws_scales, bs, Wo_words, Wo_scales, bo):
    st = f64(stack)
    hq = mxq(f64(h), 1, "e4m3")
    logits = ((hq @ unpack_weight(Wa_words, Wa_scales, FMT)) + f64(ba)).reshape(-1, NACT, S)
    e = np.exp(logits - logits.max(axis=1, keepdims=True))
    act = e / e.sum(axis=1, keepdims=True)
    top = sigmoid((hq @ unpack_weight(Ws_words, Ws_scales, FMT)) + f64(bs))[:, None, :]
    push = np.concatenate([top, st[:, :-1]], axis=1)
    empty = np.full((st.shape[0], 1, S), -1.0)
    pop = np.concatenate([st[:, 1:], empty], axis=1)
    new_stack = (push * act[:, 0][:, None, :]
                 + pop * act[:, 1][:, None, :]
                 + st * act[:, 2][:, None, :])
    out = (hq @ unpack_weight(Wo_words, Wo_scales, FMT)) + f64(bo)
    return out, new_stack

@@ -1,0 +1,307 @@
+from contextlib import ExitStack
+
+import concourse.mybir as mybir
+from concourse.masks import make_identity
+
+F32 = mybir.dt.float32
+BF16 = mybir.dt.bfloat16
+I32 = mybir.dt.int32
+U32 = mybir.dt.uint32
+U8 = mybir.dt.uint8
+FP8X4 = mybir.dt.float8_e4m3fn_x4
+ALU = mybir.AluOpType
+ACT = mybir.ActivationFunctionType
+
+P = 128
+ROWS = 4096
+K = 1024
+PASSES = K // (4 * P)
+S = 128
+DEPTH = 4
+ACTIONS = 3
+ODIM = 512
+TILES = 4
+GROUP = TILES * P
+GROUPS = ROWS // GROUP
+WA_COL = 0
+WS_COL = WA_COL + ACTIONS * S
+WO_COL = WS_COL + S
+W_COLS = WO_COL + ODIM
+
+FLOPS = 2 * ROWS * K * W_COLS
+
+
+def tile_stackrnn_pb_t_kernel(
+    tc, h, stack, Wa_words, Wa_scales, ba, Ws_words, Ws_scales, bs, Wo_words, Wo_scales, bo, out_0, out_1
+):
+    nc = tc.nc
+    with ExitStack() as pools:
+        const = pools.enter_context(tc.tile_pool(name="const", bufs=1))
+        loads = pools.enter_context(tc.tile_pool(name="loads", bufs=3))
+        work = pools.enter_context(tc.tile_pool(name="work", bufs=2))
+        small = pools.enter_context(tc.tile_pool(name="small", bufs=3))
+        psum = pools.enter_context(tc.psum_pool(name="psum", bufs=1))
+
+        def group_rows(g):
+            return slice(g * GROUP, (g + 1) * GROUP)
+
+        kept = {}
+
+        def load_h(g):
+            x = loads.tile([P, TILES, K], BF16)
+            nc.sync.dma_start(out=x[:], in_=h[group_rows(g), :].rearrange("(p t) k -> p t k", t=TILES))
+            kept["x", g] = x
+
+        def load_stack(g):
+            st = loads.tile([P, TILES, DEPTH, S], BF16)
+            nc.sync.dma_start(
+                out=st[:], in_=stack[group_rows(g)].rearrange("(p t) d s -> p t d s", t=TILES)
+            )
+            kept["st", g] = st
+
+        load_h(0)
+
+        ident = const.tile([P, P], F32)
+        make_identity(nc, ident[:])
+
+        w_words = const.tile([P, PASSES, W_COLS], U32, align_bytes=64)
+        w_planes = const.tile([P, PASSES, W_COLS], U8, align_bytes=64)
+        nc.vector.memset(w_planes[:].bitcast(I32), 0)
+        given = ((Wa_words, Wa_scales, WA_COL, ACTIONS * S), (Ws_words, Ws_scales, WS_COL, S), (Wo_words, Wo_scales, WO_COL, ODIM))
+        for words, scales, col, width in given:
+            for quad in range(4):
+                nc.sync.dma_start(
+                    out=w_planes[32 * quad : 32 * quad + 4, :, col : col + width].bitcast(I32),
+                    in_=scales[:, 4 * quad : 4 * quad + 4, :].rearrange("c r n -> r c n").bitcast(I32),
+                )
+        for words, scales, col, width in given:
+            nc.sync.dma_start(
+                out=w_words[:, :, col : col + width].bitcast(I32),
+                in_=words.rearrange("c p n t -> p c (n t)").bitcast(I32),
+            )
+
+        bo_rows = const.tile([P, ODIM], BF16)
+        nc.scalar.dma_start(out=bo_rows[:], in_=bo.partition_broadcast(P))
+
+        bias_rows = const.tile([P, P], BF16)
+        nc.vector.memset(bias_rows[:], 0.0)
+        nc.scalar.dma_start(out=bias_rows[0:ACTIONS, :], in_=ba.rearrange("(a s) -> a s", a=ACTIONS))
+        nc.scalar.dma_start(out=bias_rows[ACTIONS : ACTIONS + 1, :], in_=bs.rearrange("(a s) -> a s", a=1))
+        bias_rows_f32 = const.tile([P, P], F32)
+        nc.vector.tensor_copy(out=bias_rows_f32[:], in_=bias_rows[:])
+        bias_t = psum.tile([P, ACTIONS + 1, P], F32, tag="act_t", bufs=2)
+        nc.tensor.transpose(bias_t[:, 0, :], bias_rows_f32[:], ident[:])
+        bias_col = const.tile([P, ACTIONS + 1], F32)
+        nc.vector.tensor_copy(out=bias_col[:], in_=bias_t[:, 0, 0 : ACTIONS + 1])
+        half_bs = const.tile([P, 1], F32)
+        nc.vector.tensor_scalar_mul(out=half_bs[:], in0=bias_t[:, 0, ACTIONS : ACTIONS + 1], scalar1=0.5)
+
+        def new_quantise_input(g):
+            grouped = work.tile([P, PASSES, TILES, P, 4], BF16, align_bytes=64)
+            kept["grouped", g] = grouped
+
+        def transpose_h_tile(g, t):
+            words = kept["x", g][:, t, :].bitcast(F32)
+            h_t = psum.tile([P, PASSES, 2, P], F32, tag="h_t")
+            for c in range(PASSES):
+                for u in range(2):
+                    nc.tensor.transpose(h_t[:, c, u, :], words[:, 256 * c + u : 256 * (c + 1) : 2], ident[:])
+            nc.scalar.copy(
+                out=kept["grouped", g][:].bitcast(F32)[:, :, t, :, :],
+                in_=h_t[:].rearrange("p c u r -> p c r u"),
+            )
+
+        def quantise_h(g):
+            h_words = work.tile([P, PASSES, GROUP], U32, align_bytes=64)
+            h_planes = work.tile([P, PASSES, GROUP], U8, align_bytes=64)
+            nc.vector.quantize_mx(
+                out=h_words[:].rearrange("p c r -> p (c r)").bitcast(FP8X4),
+                scales=h_planes[:].rearrange("p c r -> p (c r)"),
+                in_=kept["grouped", g][:].rearrange("p c t r j -> p (c t r j)"),
+            )
+            kept["h_words", g] = h_words
+            kept["h_planes", g] = h_planes
+
+        def new_out_tile(g):
+            out_sb = work.tile([P, TILES, ODIM], F32)
+            kept["out_sb", g] = out_sb
+
+        def out_tile(g, t):
+            rows = slice(t * P, (t + 1) * P)
+            acc = psum.tile([P, ODIM], F32, tag="out_acc")
+            for c in range(PASSES):
+                nc.tensor.matmul_mx(
+                    out=acc[:],
+                    lhsT=kept["h_words", g][:, c, rows].bitcast(FP8X4),
+                    lhsT_scale=kept["h_planes", g][:, c, rows],
+                    rhs=w_words[:, c, WO_COL:W_COLS].bitcast(FP8X4),
+                    rhs_scale=w_planes[:, c, WO_COL:W_COLS],
+                    start=(c == 0),
+                    stop=(c == PASSES - 1),
+                )
+            nc.vector.tensor_tensor(out=kept["out_sb", g][:, t, :], in0=acc[:], in1=bo_rows[:], op=ALU.add)
+
+        def store_out(g):
+            nc.sync.dma_start(
+                out=out_0[group_rows(g), :].rearrange("(p t) n -> p t n", t=TILES), in_=kept["out_sb", g][:]
+            )
+
+        def logits(g):
+            for j in range(ACTIONS + 1):
+                acc = psum.tile([P, GROUP], F32, tag="logit%d" % j)
+                cols = slice(j * S, (j + 1) * S)
+                for c in range(PASSES):
+                    nc.tensor.matmul_mx(
+                        out=acc[:],
+                        lhsT=w_words[:, c, cols].bitcast(FP8X4),
+                        lhsT_scale=w_planes[:, c, cols],
+                        rhs=kept["h_words", g][:, c, :].bitcast(FP8X4),
+                        rhs_scale=kept["h_planes", g][:, c, :],
+                        start=(c == 0),
+                        stop=(c == PASSES - 1),
+                    )
+                kept["logit%d" % j, g] = acc
+            pop_logit = work.tile([P, GROUP], F32)
+            nc.scalar.activation(
+                out=pop_logit[:], in_=kept["logit1", g][:], func=ACT.Identity, bias=bias_col[:, 1:2], scale=1.0
+            )
+            kept["pop_logit", g] = pop_logit
+
+        def shifted_logits(g):
+            top2 = work.tile([P, GROUP], F32)
+            nc.vector.scalar_tensor_tensor(
+                out=top2[:], in0=kept["logit0", g][:], scalar=bias_col[:, 0:1], in1=kept["pop_logit", g][:],
+                op0=ALU.add, op1=ALU.max,
+            )
+            peak = work.tile([P, GROUP], F32)
+            nc.vector.scalar_tensor_tensor(
+                out=peak[:], in0=kept["logit2", g][:], scalar=bias_col[:, 2:3], in1=top2[:],
+                op0=ALU.add, op1=ALU.max,
+            )
+            z = work.tile([P, ACTIONS, GROUP], F32)
+            for i in range(ACTIONS):
+                nc.vector.scalar_tensor_tensor(
+                    out=z[:, i, :], in0=kept["logit%d" % i, g][:], scalar=bias_col[:, i : i + 1], in1=peak[:],
+                    op0=ALU.add, op1=ALU.subtract,
+                )
+            kept["z", g] = z
+            tanh_half = work.tile([P, GROUP], F32)
+            nc.scalar.activation(
+                out=tanh_half[:], in_=kept["logit3", g][:], func=ACT.Tanh, bias=half_bs[:, 0:1], scale=0.5
+            )
+            kept["tanh_half", g] = tanh_half
+
+        def exp_of_shifted(g):
+            e = work.tile([P, ACTIONS, GROUP], F32)
+            nc.scalar.activation(out=e[:], in_=kept["z", g][:], func=ACT.Exp)
+            kept["e", g] = e
+
+        def sum_of_exp(g):
+            e = kept["e", g]
+            e01 = work.tile([P, GROUP], F32)
+            nc.vector.tensor_tensor(out=e01[:], in0=e[:, 0, :], in1=e[:, 1, :], op=ALU.add)
+            total = work.tile([P, GROUP], F32)
+            nc.vector.tensor_tensor(out=total[:], in0=e01[:], in1=e[:, 2, :], op=ALU.add)
+            kept["total", g] = total
+
+        def log_weights(g):
+            log_total = work.tile([P, GROUP], F32)
+            nc.scalar.activation(out=log_total[:], in_=kept["total", g][:], func=ACT.Ln)
+            log_act = work.tile([P, ACTIONS, GROUP], F32)
+            nc.gpsimd.tensor_tensor(
+                out=log_act[:], in0=kept["z", g][:],
+                in1=log_total[:].unsqueeze(1).to_broadcast([P, ACTIONS, GROUP]), op=ALU.subtract,
+            )
+            kept["log_act", g] = log_act
+
+        def weights(g):
+            act = work.tile([P, ACTIONS + 1, GROUP], F32)
+            nc.scalar.activation(out=act[:, 0:ACTIONS, :], in_=kept["log_act", g][:], func=ACT.Exp)
+            kept["act", g] = act
+
+        def push_of_top(g):
+            act = kept["act", g]
+            nc.vector.scalar_tensor_tensor(
+                out=act[:, ACTIONS, :], in0=kept["tanh_half", g][:], scalar=1.0, in1=act[:, 0, :],
+                op0=ALU.add, op1=ALU.mult,
+            )
+
+        def new_stack_tile(g):
+            new_sb = work.tile([P, TILES, DEPTH, S], F32)
+            kept["new_sb", g] = new_sb
+
+        def transpose_weights(g, t):
+            act_t = psum.tile([P, ACTIONS + 1, P], F32, tag="act_t", bufs=2)
+            for j in range(ACTIONS + 1):
+                nc.tensor.transpose(act_t[:, j, :], kept["act", g][:, j, t * P : (t + 1) * P], ident[:])
+            kept["act_t", g, t] = act_t
+
+        def blend_tile(g, t):
+            st = kept["st", g][:, t, :, :]
+            new = kept["new_sb", g][:, t, :, :]
+            act_t = kept["act_t", g, t]
+
+            def over_depth(j, depth):
+                return act_t[:, j, :].unsqueeze(1).to_broadcast([P, depth, S])
+
+            nc.vector.tensor_tensor(out=new, in0=st, in1=over_depth(2, DEPTH), op=ALU.mult)
+            pushed = small.tile([P, DEPTH - 1, S], F32)
+            nc.vector.tensor_tensor(out=pushed[:], in0=st[:, 0 : DEPTH - 1, :], in1=over_depth(0, DEPTH - 1), op=ALU.mult)
+            popped = small.tile([P, DEPTH - 1, S], F32)
+            nc.vector.tensor_tensor(out=popped[:], in0=st[:, 1:DEPTH, :], in1=over_depth(1, DEPTH - 1), op=ALU.mult)
+            nc.vector.scalar_tensor_tensor(
+                out=new[:, 0, :], in0=act_t[:, ACTIONS, :], scalar=0.5, in1=new[:, 0, :], op0=ALU.mult, op1=ALU.add
+            )
+            nc.vector.tensor_tensor(out=new[:, DEPTH - 1, :], in0=new[:, DEPTH - 1, :], in1=act_t[:, 1, :], op=ALU.subtract)
+            nc.gpsimd.tensor_tensor(out=new[:, 1:DEPTH, :], in0=new[:, 1:DEPTH, :], in1=pushed[:], op=ALU.add)
+            nc.gpsimd.tensor_tensor(out=new[:, 0 : DEPTH - 1, :], in0=new[:, 0 : DEPTH - 1, :], in1=popped[:], op=ALU.add)
+
+        def store_new_stack(g):
+            nc.sync.dma_start(
+                out=out_1[group_rows(g)].rearrange("(p t) d s -> p t d s", t=TILES), in_=kept["new_sb", g][:]
+            )
+
+        def live(g):
+            return 0 <= g < GROUPS
+
+        for r in range(-2, GROUPS + 1):
+            if live(r + 3):
+                load_h(r + 3)
+            if live(r + 1):
+                load_stack(r + 1)
+            if live(r):
+                log_weights(r)
+            if live(r - 1):
+                new_stack_tile(r - 1)
+                transpose_weights(r - 1, 0)
+                transpose_weights(r - 1, 1)
+            if live(r + 1):
+                logits(r + 1)
+                new_out_tile(r + 1)
+            if live(r + 2):
+                new_quantise_input(r + 2)
+            for t in range(TILES):
+                if live(r - 1):
+                    blend_tile(r - 1, t)
+                if live(r + 1):
+                    out_tile(r + 1, t)
+                if live(r + 2):
+                    transpose_h_tile(r + 2, t)
+                if live(r - 1) and t + 2 < TILES:
+                    transpose_weights(r - 1, t + 2)
+                if t == 1:
+                    if live(r + 1):
+                        shifted_logits(r + 1)
+                    if live(r):
+                        weights(r)
+                    if live(r + 1):
+                        exp_of_shifted(r + 1)
+            if live(r + 1):
+                store_out(r + 1)
+                sum_of_exp(r + 1)
+            if live(r):
+                push_of_top(r)
+            if live(r + 2):
+                quantise_h(r + 2)
+            if live(r - 1):
+                store_new_stack(r - 1)

@@ -21,6 +21,7 @@ DEPTH = 4
 ACTIONS = 3
 ODIM = 512
 TILES = 4
+PAIR = 2
 GROUP = TILES * P
 GROUPS = ROWS // GROUP
 WA_COL = 0
@@ -39,7 +40,7 @@ def tile_stackrnn_pb_t_kernel(
         const = pools.enter_context(tc.tile_pool(name="const", bufs=1))
         loads = pools.enter_context(tc.tile_pool(name="loads", bufs=3))
         work = pools.enter_context(tc.tile_pool(name="work", bufs=2))
-        small = pools.enter_context(tc.tile_pool(name="small", bufs=3))
+        small = pools.enter_context(tc.tile_pool(name="small", bufs=2))
         psum = pools.enter_context(tc.psum_pool(name="psum", bufs=1))
 
         def group_rows(g):
@@ -49,7 +50,9 @@ def tile_stackrnn_pb_t_kernel(
 
         def load_h(g):
             x = loads.tile([P, TILES, K], BF16)
-            nc.sync.dma_start(out=x[:], in_=h[group_rows(g), :].rearrange("(p t) k -> p t k", t=TILES))
+            rows = h[group_rows(g), :].rearrange("(p t) k -> p t k", t=TILES)
+            for t in range(TILES):
+                nc.sync.dma_start(out=x[:, t, :], in_=rows[:, t, :])
             kept["x", g] = x
 
         def load_stack(g):
@@ -89,7 +92,7 @@ def tile_stackrnn_pb_t_kernel(
         nc.scalar.dma_start(out=bias_rows[ACTIONS : ACTIONS + 1, :], in_=bs.rearrange("(a s) -> a s", a=1))
         bias_rows_f32 = const.tile([P, P], F32)
         nc.vector.tensor_copy(out=bias_rows_f32[:], in_=bias_rows[:])
-        bias_t = psum.tile([P, ACTIONS + 1, P], F32, tag="act_t", bufs=2)
+        bias_t = psum.tile([P, ACTIONS + 1, P], F32, tag="noop_push")
         nc.tensor.transpose(bias_t[:, 0, :], bias_rows_f32[:], ident[:])
         bias_col = const.tile([P, ACTIONS + 1], F32)
         nc.vector.tensor_copy(out=bias_col[:], in_=bias_t[:, 0, 0 : ACTIONS + 1])
@@ -141,9 +144,11 @@ def tile_stackrnn_pb_t_kernel(
                 )
             nc.vector.tensor_tensor(out=kept["out_sb", g][:, t, :], in0=acc[:], in1=bo_rows[:], op=ALU.add)
 
-        def store_out(g):
+        def store_out(g, pair):
+            tiles = slice(pair * PAIR, (pair + 1) * PAIR)
             nc.sync.dma_start(
-                out=out_0[group_rows(g), :].rearrange("(p t) n -> p t n", t=TILES), in_=kept["out_sb", g][:]
+                out=out_0[group_rows(g), :].rearrange("(p t) n -> p t n", t=TILES)[:, tiles, :],
+                in_=kept["out_sb", g][:, tiles, :],
             )
 
         def logits(g):
@@ -230,35 +235,49 @@ def tile_stackrnn_pb_t_kernel(
             new_sb = work.tile([P, TILES, DEPTH, S], F32)
             kept["new_sb", g] = new_sb
 
-        def transpose_weights(g, t):
-            act_t = psum.tile([P, ACTIONS + 1, P], F32, tag="act_t", bufs=2)
-            for j in range(ACTIONS + 1):
-                nc.tensor.transpose(act_t[:, j, :], kept["act", g][:, j, t * P : (t + 1) * P], ident[:])
-            kept["act_t", g, t] = act_t
+        def transpose_weights(g, pair):
+            act = kept["act", g]
+            noop_push = psum.tile([P, 2, PAIR, S], F32, tag="noop_push")
+            pop_top = psum.tile([P, 2, PAIR, S], F32, tag="pop_top")
+            for bank, planes in ((noop_push, (2, 0)), (pop_top, (1, ACTIONS))):
+                for k, j in enumerate(planes):
+                    for i in range(PAIR):
+                        t = pair * PAIR + i
+                        nc.tensor.transpose(bank[:, k, i, :], act[:, j, t * P : (t + 1) * P], ident[:])
+            kept["noop_push", g, pair] = noop_push
+            kept["pop_top", g, pair] = pop_top
 
-        def blend_tile(g, t):
-            st = kept["st", g][:, t, :, :]
-            new = kept["new_sb", g][:, t, :, :]
-            act_t = kept["act_t", g, t]
+        def blend_pair(g, pair):
+            tiles = slice(pair * PAIR, (pair + 1) * PAIR)
+            st = kept["st", g][:, tiles, :, :]
+            new = kept["new_sb", g][:, tiles, :, :]
+            noop_push = kept["noop_push", g, pair]
+            pop_top = kept["pop_top", g, pair]
 
-            def over_depth(j, depth):
-                return act_t[:, j, :].unsqueeze(1).to_broadcast([P, depth, S])
+            def over_depth(plane, depth):
+                return plane.unsqueeze(2).to_broadcast([P, PAIR, depth, S])
 
-            nc.vector.tensor_tensor(out=new, in0=st, in1=over_depth(2, DEPTH), op=ALU.mult)
-            pushed = small.tile([P, DEPTH - 1, S], F32)
-            nc.vector.tensor_tensor(out=pushed[:], in0=st[:, 0 : DEPTH - 1, :], in1=over_depth(0, DEPTH - 1), op=ALU.mult)
-            popped = small.tile([P, DEPTH - 1, S], F32)
-            nc.vector.tensor_tensor(out=popped[:], in0=st[:, 1:DEPTH, :], in1=over_depth(1, DEPTH - 1), op=ALU.mult)
-            nc.vector.scalar_tensor_tensor(
-                out=new[:, 0, :], in0=act_t[:, ACTIONS, :], scalar=0.5, in1=new[:, 0, :], op0=ALU.mult, op1=ALU.add
+            nc.vector.tensor_tensor(out=new, in0=st, in1=over_depth(noop_push[:, 0, :, :], DEPTH), op=ALU.mult)
+            pushed = small.tile([P, PAIR, DEPTH - 1, S], F32)
+            nc.vector.tensor_tensor(
+                out=pushed[:], in0=st[:, :, 0 : DEPTH - 1, :], in1=over_depth(noop_push[:, 1, :, :], DEPTH - 1), op=ALU.mult
             )
-            nc.vector.tensor_tensor(out=new[:, DEPTH - 1, :], in0=new[:, DEPTH - 1, :], in1=act_t[:, 1, :], op=ALU.subtract)
-            nc.gpsimd.tensor_tensor(out=new[:, 1:DEPTH, :], in0=new[:, 1:DEPTH, :], in1=pushed[:], op=ALU.add)
-            nc.gpsimd.tensor_tensor(out=new[:, 0 : DEPTH - 1, :], in0=new[:, 0 : DEPTH - 1, :], in1=popped[:], op=ALU.add)
-
-        def store_new_stack(g):
+            popped = small.tile([P, PAIR, DEPTH - 1, S], F32)
+            nc.vector.tensor_tensor(
+                out=popped[:], in0=st[:, :, 1:DEPTH, :], in1=over_depth(pop_top[:, 0, :, :], DEPTH - 1), op=ALU.mult
+            )
+            nc.vector.scalar_tensor_tensor(
+                out=new[:, :, 0, :], in0=pop_top[:, 1, :, :], scalar=0.5, in1=new[:, :, 0, :], op0=ALU.mult, op1=ALU.add
+            )
+            nc.vector.tensor_tensor(
+                out=new[:, :, DEPTH - 1, :], in0=new[:, :, DEPTH - 1, :], in1=pop_top[:, 0, :, :], op=ALU.subtract
+            )
+            nc.gpsimd.tensor_tensor(out=new[:, :, 1:DEPTH, :], in0=new[:, :, 1:DEPTH, :], in1=pushed[:], op=ALU.add)
+            nc.gpsimd.tensor_tensor(
+                out=new[:, :, 0 : DEPTH - 1, :], in0=new[:, :, 0 : DEPTH - 1, :], in1=popped[:], op=ALU.add
+            )
             nc.sync.dma_start(
-                out=out_1[group_rows(g)].rearrange("(p t) d s -> p t d s", t=TILES), in_=kept["new_sb", g][:]
+                out=out_1[group_rows(g)].rearrange("(p t) d s -> p t d s", t=TILES)[:, tiles, :, :], in_=new
             )
 
         def live(g):
@@ -274,34 +293,32 @@ def tile_stackrnn_pb_t_kernel(
             if live(r - 1):
                 new_stack_tile(r - 1)
                 transpose_weights(r - 1, 0)
-                transpose_weights(r - 1, 1)
             if live(r + 1):
                 logits(r + 1)
                 new_out_tile(r + 1)
             if live(r + 2):
                 new_quantise_input(r + 2)
-            for t in range(TILES):
+            for pair in range(TILES // PAIR):
                 if live(r - 1):
-                    blend_tile(r - 1, t)
+                    blend_pair(r - 1, pair)
+                for t in range(pair * PAIR, (pair + 1) * PAIR):
+                    if live(r + 1):
+                        out_tile(r + 1, t)
+                    if live(r + 2):
+                        transpose_h_tile(r + 2, t)
                 if live(r + 1):
-                    out_tile(r + 1, t)
-                if live(r + 2):
-                    transpose_h_tile(r + 2, t)
-                if live(r - 1) and t + 2 < TILES:
-                    transpose_weights(r - 1, t + 2)
-                if t == 1:
+                    store_out(r + 1, pair)
+                if pair == 0:
+                    if live(r - 1):
+                        transpose_weights(r - 1, 1)
                     if live(r + 1):
                         shifted_logits(r + 1)
                     if live(r):
                         weights(r)
                     if live(r + 1):
                         exp_of_shifted(r + 1)
-            if live(r + 1):
-                store_out(r + 1)
-                sum_of_exp(r + 1)
+                        sum_of_exp(r + 1)
             if live(r):
                 push_of_top(r)
             if live(r + 2):
                 quantise_h(r + 2)
-            if live(r - 1):
-                store_new_stack(r - 1)

@@ -21,7 +21,6 @@ DEPTH = 4
 ACTIONS = 3
 ODIM = 512
 TILES = 4
-PAIR = 2
 GROUP = TILES * P
 GROUPS = ROWS // GROUP
 WA_COL = 0
@@ -40,8 +39,9 @@ def tile_stackrnn_pb_t_kernel(
         const = pools.enter_context(tc.tile_pool(name="const", bufs=1))
         loads = pools.enter_context(tc.tile_pool(name="loads", bufs=3))
         work = pools.enter_context(tc.tile_pool(name="work", bufs=2))
-        small = pools.enter_context(tc.tile_pool(name="small", bufs=2))
+        small = pools.enter_context(tc.tile_pool(name="small", bufs=3))
         psum = pools.enter_context(tc.psum_pool(name="psum", bufs=1))
+        pools.enter_context(tc.manual_schedule())
 
         def group_rows(g):
             return slice(g * GROUP, (g + 1) * GROUP)
@@ -91,13 +91,15 @@ def tile_stackrnn_pb_t_kernel(
         nc.scalar.dma_start(out=bias_rows[0:ACTIONS, :], in_=ba.rearrange("(a s) -> a s", a=ACTIONS))
         nc.scalar.dma_start(out=bias_rows[ACTIONS : ACTIONS + 1, :], in_=bs.rearrange("(a s) -> a s", a=1))
         bias_rows_f32 = const.tile([P, P], F32)
-        nc.vector.tensor_copy(out=bias_rows_f32[:], in_=bias_rows[:])
-        bias_t = psum.tile([P, ACTIONS + 1, P], F32, tag="noop_push")
-        nc.tensor.transpose(bias_t[:, 0, :], bias_rows_f32[:], ident[:])
         bias_col = const.tile([P, ACTIONS + 1], F32)
-        nc.vector.tensor_copy(out=bias_col[:], in_=bias_t[:, 0, 0 : ACTIONS + 1])
         half_bs = const.tile([P, 1], F32)
-        nc.vector.tensor_scalar_mul(out=half_bs[:], in0=bias_t[:, 0, ACTIONS : ACTIONS + 1], scalar1=0.5)
+
+        def turn_biases():
+            nc.vector.tensor_copy(out=bias_rows_f32[:], in_=bias_rows[:])
+            bias_t = psum.tile([P, ACTIONS + 1, P], F32, tag="act_t", bufs=2)
+            nc.tensor.transpose(bias_t[:, 0, :], bias_rows_f32[:], ident[:])
+            nc.vector.tensor_copy(out=bias_col[:], in_=bias_t[:, 0, 0 : ACTIONS + 1])
+            nc.vector.tensor_scalar_mul(out=half_bs[:], in0=bias_t[:, 0, ACTIONS : ACTIONS + 1], scalar1=0.5)
 
         def new_quantise_input(g):
             grouped = work.tile([P, PASSES, TILES, P, 4], BF16, align_bytes=64)
@@ -105,7 +107,7 @@ def tile_stackrnn_pb_t_kernel(
 
         def transpose_h_tile(g, t):
             words = kept["x", g][:, t, :].bitcast(F32)
-            h_t = psum.tile([P, PASSES, 2, P], F32, tag="h_t")
+            h_t = psum.tile([P, PASSES, 2, P], F32, tag="turn", bufs=2)
             for c in range(PASSES):
                 for u in range(2):
                     nc.tensor.transpose(h_t[:, c, u, :], words[:, 256 * c + u : 256 * (c + 1) : 2], ident[:])
@@ -129,9 +131,9 @@ def tile_stackrnn_pb_t_kernel(
             out_sb = work.tile([P, TILES, ODIM], F32)
             kept["out_sb", g] = out_sb
 
-        def out_tile(g, t):
+        def out_passes(g, t):
             rows = slice(t * P, (t + 1) * P)
-            acc = psum.tile([P, ODIM], F32, tag="out_acc")
+            acc = psum.tile([P, ODIM], F32, tag="turn", bufs=2)
             for c in range(PASSES):
                 nc.tensor.matmul_mx(
                     out=acc[:],
@@ -142,13 +144,16 @@ def tile_stackrnn_pb_t_kernel(
                     start=(c == 0),
                     stop=(c == PASSES - 1),
                 )
-            nc.vector.tensor_tensor(out=kept["out_sb", g][:, t, :], in0=acc[:], in1=bo_rows[:], op=ALU.add)
+            kept["out_acc", g, t] = acc
 
-        def store_out(g, pair):
-            tiles = slice(pair * PAIR, (pair + 1) * PAIR)
+        def out_bias(g, t):
+            nc.vector.tensor_tensor(
+                out=kept["out_sb", g][:, t, :], in0=kept["out_acc", g, t][:], in1=bo_rows[:], op=ALU.add
+            )
+
+        def store_out(g):
             nc.sync.dma_start(
-                out=out_0[group_rows(g), :].rearrange("(p t) n -> p t n", t=TILES)[:, tiles, :],
-                in_=kept["out_sb", g][:, tiles, :],
+                out=out_0[group_rows(g), :].rearrange("(p t) n -> p t n", t=TILES), in_=kept["out_sb", g][:]
             )
 
         def logits(g):
@@ -172,7 +177,7 @@ def tile_stackrnn_pb_t_kernel(
             )
             kept["pop_logit", g] = pop_logit
 
-        def shifted_logits(g):
+        def peak_of_logits(g):
             top2 = work.tile([P, GROUP], F32)
             nc.vector.scalar_tensor_tensor(
                 out=top2[:], in0=kept["logit0", g][:], scalar=bias_col[:, 0:1], in1=kept["pop_logit", g][:],
@@ -183,6 +188,10 @@ def tile_stackrnn_pb_t_kernel(
                 out=peak[:], in0=kept["logit2", g][:], scalar=bias_col[:, 2:3], in1=top2[:],
                 op0=ALU.add, op1=ALU.max,
             )
+            kept["peak", g] = peak
+
+        def shifted_logits(g):
+            peak = kept["peak", g]
             z = work.tile([P, ACTIONS, GROUP], F32)
             for i in range(ACTIONS):
                 nc.vector.scalar_tensor_tensor(
@@ -190,6 +199,8 @@ def tile_stackrnn_pb_t_kernel(
                     op0=ALU.add, op1=ALU.subtract,
                 )
             kept["z", g] = z
+
+        def tanh_of_top(g):
             tanh_half = work.tile([P, GROUP], F32)
             nc.scalar.activation(
                 out=tanh_half[:], in_=kept["logit3", g][:], func=ACT.Tanh, bias=half_bs[:, 0:1], scale=0.5
@@ -201,21 +212,24 @@ def tile_stackrnn_pb_t_kernel(
             nc.scalar.activation(out=e[:], in_=kept["z", g][:], func=ACT.Exp)
             kept["e", g] = e
 
-        def sum_of_exp(g):
+        def sum_first_two(g):
             e = kept["e", g]
             e01 = work.tile([P, GROUP], F32)
             nc.vector.tensor_tensor(out=e01[:], in0=e[:, 0, :], in1=e[:, 1, :], op=ALU.add)
+            kept["e01", g] = e01
+
+        def log_of_sum(g):
             total = work.tile([P, GROUP], F32)
-            nc.vector.tensor_tensor(out=total[:], in0=e01[:], in1=e[:, 2, :], op=ALU.add)
-            kept["total", g] = total
+            nc.vector.tensor_tensor(out=total[:], in0=kept["e01", g][:], in1=kept["e", g][:, 2, :], op=ALU.add)
+            log_total = work.tile([P, GROUP], F32)
+            nc.scalar.activation(out=log_total[:], in_=total[:], func=ACT.Ln)
+            kept["log_total", g] = log_total
 
         def log_weights(g):
-            log_total = work.tile([P, GROUP], F32)
-            nc.scalar.activation(out=log_total[:], in_=kept["total", g][:], func=ACT.Ln)
             log_act = work.tile([P, ACTIONS, GROUP], F32)
             nc.gpsimd.tensor_tensor(
                 out=log_act[:], in0=kept["z", g][:],
-                in1=log_total[:].unsqueeze(1).to_broadcast([P, ACTIONS, GROUP]), op=ALU.subtract,
+                in1=kept["log_total", g][:].unsqueeze(1).to_broadcast([P, ACTIONS, GROUP]), op=ALU.subtract,
             )
             kept["log_act", g] = log_act
 
@@ -235,90 +249,79 @@ def tile_stackrnn_pb_t_kernel(
             new_sb = work.tile([P, TILES, DEPTH, S], F32)
             kept["new_sb", g] = new_sb
 
-        def transpose_weights(g, pair):
-            act = kept["act", g]
-            noop_push = psum.tile([P, 2, PAIR, S], F32, tag="noop_push")
-            pop_top = psum.tile([P, 2, PAIR, S], F32, tag="pop_top")
-            for bank, planes in ((noop_push, (2, 0)), (pop_top, (1, ACTIONS))):
-                for k, j in enumerate(planes):
-                    for i in range(PAIR):
-                        t = pair * PAIR + i
-                        nc.tensor.transpose(bank[:, k, i, :], act[:, j, t * P : (t + 1) * P], ident[:])
-            kept["noop_push", g, pair] = noop_push
-            kept["pop_top", g, pair] = pop_top
+        def transpose_weights(g, t):
+            act_t = psum.tile([P, ACTIONS + 1, P], F32, tag="act_t", bufs=2)
+            for j in range(ACTIONS + 1):
+                nc.tensor.transpose(act_t[:, j, :], kept["act", g][:, j, t * P : (t + 1) * P], ident[:])
+            kept["act_t", g, t] = act_t
 
-        def blend_pair(g, pair):
-            tiles = slice(pair * PAIR, (pair + 1) * PAIR)
-            st = kept["st", g][:, tiles, :, :]
-            new = kept["new_sb", g][:, tiles, :, :]
-            noop_push = kept["noop_push", g, pair]
-            pop_top = kept["pop_top", g, pair]
+        def blend_tile(g, t):
+            st = kept["st", g][:, t, :, :]
+            new = kept["new_sb", g][:, t, :, :]
+            act_t = kept["act_t", g, t]
 
-            def over_depth(plane, depth):
-                return plane.unsqueeze(2).to_broadcast([P, PAIR, depth, S])
+            def over_depth(j, depth):
+                return act_t[:, j, :].unsqueeze(1).to_broadcast([P, depth, S])
 
-            nc.vector.tensor_tensor(out=new, in0=st, in1=over_depth(noop_push[:, 0, :, :], DEPTH), op=ALU.mult)
-            pushed = small.tile([P, PAIR, DEPTH - 1, S], F32)
-            nc.vector.tensor_tensor(
-                out=pushed[:], in0=st[:, :, 0 : DEPTH - 1, :], in1=over_depth(noop_push[:, 1, :, :], DEPTH - 1), op=ALU.mult
-            )
-            popped = small.tile([P, PAIR, DEPTH - 1, S], F32)
-            nc.vector.tensor_tensor(
-                out=popped[:], in0=st[:, :, 1:DEPTH, :], in1=over_depth(pop_top[:, 0, :, :], DEPTH - 1), op=ALU.mult
-            )
+            nc.vector.tensor_tensor(out=new, in0=st, in1=over_depth(2, DEPTH), op=ALU.mult)
+            pushed = small.tile([P, DEPTH - 1, S], F32)
+            nc.vector.tensor_tensor(out=pushed[:], in0=st[:, 0 : DEPTH - 1, :], in1=over_depth(0, DEPTH - 1), op=ALU.mult)
+            popped = small.tile([P, DEPTH - 1, S], F32)
+            nc.vector.tensor_tensor(out=popped[:], in0=st[:, 1:DEPTH, :], in1=over_depth(1, DEPTH - 1), op=ALU.mult)
             nc.vector.scalar_tensor_tensor(
-                out=new[:, :, 0, :], in0=pop_top[:, 1, :, :], scalar=0.5, in1=new[:, :, 0, :], op0=ALU.mult, op1=ALU.add
+                out=new[:, 0, :], in0=act_t[:, ACTIONS, :], scalar=0.5, in1=new[:, 0, :], op0=ALU.mult, op1=ALU.add
             )
-            nc.vector.tensor_tensor(
-                out=new[:, :, DEPTH - 1, :], in0=new[:, :, DEPTH - 1, :], in1=pop_top[:, 0, :, :], op=ALU.subtract
-            )
-            nc.gpsimd.tensor_tensor(out=new[:, :, 1:DEPTH, :], in0=new[:, :, 1:DEPTH, :], in1=pushed[:], op=ALU.add)
-            nc.gpsimd.tensor_tensor(
-                out=new[:, :, 0 : DEPTH - 1, :], in0=new[:, :, 0 : DEPTH - 1, :], in1=popped[:], op=ALU.add
-            )
-            nc.sync.dma_start(
-                out=out_1[group_rows(g)].rearrange("(p t) d s -> p t d s", t=TILES)[:, tiles, :, :], in_=new
-            )
+            nc.vector.tensor_tensor(out=new[:, DEPTH - 1, :], in0=new[:, DEPTH - 1, :], in1=act_t[:, 1, :], op=ALU.subtract)
+            nc.gpsimd.tensor_tensor(out=new[:, 1:DEPTH, :], in0=new[:, 1:DEPTH, :], in1=pushed[:], op=ALU.add)
+            nc.gpsimd.tensor_tensor(out=new[:, 0 : DEPTH - 1, :], in0=new[:, 0 : DEPTH - 1, :], in1=popped[:], op=ALU.add)
+            nc.sync.dma_start(out=out_1[group_rows(g)].rearrange("(p t) d s -> p t d s", t=TILES)[:, t, :, :], in_=new)
 
         def live(g):
             return 0 <= g < GROUPS
 
+        def stage(g, step, *args):
+            if live(g):
+                step(g, *args)
+
+        load_h(1)
+        new_quantise_input(0)
+        transpose_h_tile(0, 0)
+        turn_biases()
         for r in range(-2, GROUPS + 1):
-            if live(r + 3):
-                load_h(r + 3)
-            if live(r + 1):
-                load_stack(r + 1)
-            if live(r):
-                log_weights(r)
-            if live(r - 1):
-                new_stack_tile(r - 1)
-                transpose_weights(r - 1, 0)
-            if live(r + 1):
-                logits(r + 1)
-                new_out_tile(r + 1)
-            if live(r + 2):
-                new_quantise_input(r + 2)
-            for pair in range(TILES // PAIR):
-                if live(r - 1):
-                    blend_pair(r - 1, pair)
-                for t in range(pair * PAIR, (pair + 1) * PAIR):
-                    if live(r + 1):
-                        out_tile(r + 1, t)
-                    if live(r + 2):
-                        transpose_h_tile(r + 2, t)
-                if live(r + 1):
-                    store_out(r + 1, pair)
-                if pair == 0:
-                    if live(r - 1):
-                        transpose_weights(r - 1, 1)
-                    if live(r + 1):
-                        shifted_logits(r + 1)
-                    if live(r):
-                        weights(r)
-                    if live(r + 1):
-                        exp_of_shifted(r + 1)
-                        sum_of_exp(r + 1)
-            if live(r):
-                push_of_top(r)
-            if live(r + 2):
-                quantise_h(r + 2)
+            stage(r + 4, load_h)
+            stage(r + 1, load_stack)
+            stage(r, log_weights)
+            stage(r - 1, new_stack_tile)
+            stage(r + 1, logits)
+            stage(r + 1, new_out_tile)
+            stage(r + 1, out_passes, 0)
+            stage(r - 1, blend_tile, 0)
+            stage(r - 1, transpose_weights, 2)
+            stage(r + 2, transpose_h_tile, 1)
+            stage(r - 1, blend_tile, 1)
+            stage(r - 1, transpose_weights, 3)
+            stage(r + 1, tanh_of_top)
+            stage(r, weights)
+            stage(r + 2, transpose_h_tile, 2)
+            stage(r + 1, peak_of_logits)
+            stage(r + 1, out_bias, 0)
+            stage(r + 1, out_passes, 1)
+            stage(r + 1, shifted_logits)
+            stage(r + 1, exp_of_shifted)
+            stage(r + 2, transpose_h_tile, 3)
+            stage(r - 1, blend_tile, 2)
+            stage(r + 1, out_bias, 1)
+            stage(r + 1, out_passes, 2)
+            stage(r - 1, blend_tile, 3)
+            stage(r, push_of_top)
+            stage(r, transpose_weights, 0)
+            stage(r, transpose_weights, 1)
+            stage(r + 1, out_bias, 2)
+            stage(r + 1, out_passes, 3)
+            stage(r + 1, sum_first_two)
+            stage(r + 2, quantise_h)
+            stage(r + 1, log_of_sum)
+            stage(r + 1, out_bias, 3)
+            stage(r + 1, store_out)
+            stage(r + 3, new_quantise_input)
+            stage(r + 3, transpose_h_tile, 0)

@@ -295,16 +295,16 @@ def tile_stackrnn_pb_t_kernel(
             stage(r + 1, logits)
             stage(r + 1, new_out_tile)
             stage(r + 1, out_passes, 0)
+            stage(r + 1, tanh_of_top)
             stage(r - 1, blend_tile, 0)
             stage(r - 1, transpose_weights, 2)
             stage(r + 2, transpose_h_tile, 1)
             stage(r - 1, blend_tile, 1)
             stage(r - 1, transpose_weights, 3)
-            stage(r + 1, tanh_of_top)
             stage(r, weights)
-            stage(r + 2, transpose_h_tile, 2)
             stage(r + 1, peak_of_logits)
             stage(r + 1, out_bias, 0)
+            stage(r + 2, transpose_h_tile, 2)
             stage(r + 1, out_passes, 1)
             stage(r + 1, shifted_logits)
             stage(r + 1, exp_of_shifted)
@@ -313,12 +313,12 @@ def tile_stackrnn_pb_t_kernel(
             stage(r + 1, out_bias, 1)
             stage(r + 1, out_passes, 2)
             stage(r - 1, blend_tile, 3)
+            stage(r + 1, out_passes, 3)
             stage(r, push_of_top)
             stage(r, transpose_weights, 0)
             stage(r, transpose_weights, 1)
-            stage(r + 1, out_bias, 2)
-            stage(r + 1, out_passes, 3)
             stage(r + 1, sum_first_two)
+            stage(r + 1, out_bias, 2)
             stage(r + 2, quantise_h)
             stage(r + 1, log_of_sum)
             stage(r + 1, out_bias, 3)

@@ -31,6 +31,10 @@ W_COLS = WO_COL + ODIM
 FLOPS = 2 * ROWS * K * W_COLS
 
 
+def vector_adds(g, t):
+    return g == GROUPS - 1
+
+
 def tile_stackrnn_pb_t_kernel(
     tc, h, stack, Wa_words, Wa_scales, ba, Ws_words, Ws_scales, bs, Wo_words, Wo_scales, bo, out_0, out_1
 ):
@@ -272,7 +276,8 @@ def tile_stackrnn_pb_t_kernel(
                 out=new[:, 0, :], in0=act_t[:, ACTIONS, :], scalar=0.5, in1=new[:, 0, :], op0=ALU.mult, op1=ALU.add
             )
             nc.vector.tensor_tensor(out=new[:, DEPTH - 1, :], in0=new[:, DEPTH - 1, :], in1=act_t[:, 1, :], op=ALU.subtract)
-            nc.gpsimd.tensor_tensor(out=new[:, 1:DEPTH, :], in0=new[:, 1:DEPTH, :], in1=pushed[:], op=ALU.add)
+            adder = nc.vector if vector_adds(g, t) else nc.gpsimd
+            adder.tensor_tensor(out=new[:, 1:DEPTH, :], in0=new[:, 1:DEPTH, :], in1=pushed[:], op=ALU.add)
             nc.gpsimd.tensor_tensor(out=new[:, 0 : DEPTH - 1, :], in0=new[:, 0 : DEPTH - 1, :], in1=popped[:], op=ALU.add)
             nc.sync.dma_start(out=out_1[group_rows(g)].rearrange("(p t) d s -> p t d s", t=TILES)[:, t, :, :], in_=new)
 
@@ -285,9 +290,14 @@ def tile_stackrnn_pb_t_kernel(
 
         load_h(1)
         new_quantise_input(0)
-        transpose_h_tile(0, 0)
+        for t in range(TILES):
+            transpose_h_tile(0, t)
+        load_h(2)
+        quantise_h(0)
+        new_quantise_input(1)
+        transpose_h_tile(1, 0)
         turn_biases()
-        for r in range(-2, GROUPS + 1):
+        for r in range(-1, GROUPS + 1):
             stage(r + 4, load_h)
             stage(r + 1, load_stack)
             stage(r, log_weights)

@@ -87,8 +87,12 @@ def tile_stackrnn_pb_t_kernel(
                 in_=words.rearrange("c p n t -> p c (n t)").bitcast(I32),
             )
 
-        bo_rows = const.tile([P, ODIM], BF16)
-        nc.scalar.dma_start(out=bo_rows[:], in_=bo.partition_broadcast(P))
+        bo_alone = const.tile([P, ODIM], BF16)
+        nc.vector.memset(bo_alone[:], 0.0)
+        nc.scalar.dma_start(out=bo_alone[0:1, :], in_=bo.rearrange("(a n) -> a n", a=1))
+        ones = const.tile([P, P], BF16)
+        nc.vector.memset(ones[:], 1.0)
+        bo_rows = const.tile([P, ODIM], F32)
 
         bias_rows = const.tile([P, P], BF16)
         nc.vector.memset(bias_rows[:], 0.0)
@@ -104,6 +108,9 @@ def tile_stackrnn_pb_t_kernel(
             nc.tensor.transpose(bias_t[:, 0, :], bias_rows_f32[:], ident[:])
             nc.vector.tensor_copy(out=bias_col[:], in_=bias_t[:, 0, 0 : ACTIONS + 1])
             nc.vector.tensor_scalar_mul(out=half_bs[:], in0=bias_t[:, 0, ACTIONS : ACTIONS + 1], scalar1=0.5)
+            bo_spread = psum.tile([P, ODIM], F32, tag="act_t", bufs=2)
+            nc.tensor.matmul(out=bo_spread[:], lhsT=ones[:], rhs=bo_alone[:], start=True, stop=True)
+            nc.vector.tensor_copy(out=bo_rows[:], in_=bo_spread[:])
 
         def new_quantise_input(g):
             grouped = work.tile([P, PASSES, TILES, P, 4], BF16, align_bytes=64)
@@ -181,15 +188,18 @@ def tile_stackrnn_pb_t_kernel(
             )
             kept["pop_logit", g] = pop_logit
 
-        def peak_of_logits(g):
+        def peak_first(g):
             top2 = work.tile([P, GROUP], F32)
             nc.vector.scalar_tensor_tensor(
                 out=top2[:], in0=kept["logit0", g][:], scalar=bias_col[:, 0:1], in1=kept["pop_logit", g][:],
                 op0=ALU.add, op1=ALU.max,
             )
+            kept["top2", g] = top2
+
+        def peak_second(g):
             peak = work.tile([P, GROUP], F32)
             nc.vector.scalar_tensor_tensor(
-                out=peak[:], in0=kept["logit2", g][:], scalar=bias_col[:, 2:3], in1=top2[:],
+                out=peak[:], in0=kept["logit2", g][:], scalar=bias_col[:, 2:3], in1=kept["top2", g][:],
                 op0=ALU.add, op1=ALU.max,
             )
             kept["peak", g] = peak
@@ -312,14 +322,15 @@ def tile_stackrnn_pb_t_kernel(
             stage(r - 1, blend_tile, 1)
             stage(r - 1, transpose_weights, 3)
             stage(r, weights)
-            stage(r + 1, peak_of_logits)
+            stage(r + 1, peak_first)
             stage(r + 1, out_bias, 0)
             stage(r + 2, transpose_h_tile, 2)
             stage(r + 1, out_passes, 1)
+            stage(r + 1, peak_second)
+            stage(r - 1, blend_tile, 2)
             stage(r + 1, shifted_logits)
             stage(r + 1, exp_of_shifted)
             stage(r + 2, transpose_h_tile, 3)
-            stage(r - 1, blend_tile, 2)
             stage(r + 1, out_bias, 1)
             stage(r + 1, out_passes, 2)
             stage(r - 1, blend_tile, 3)

@@ -118,7 +118,8 @@ def tile_stackrnn_pb_t_kernel(
 
         def transpose_h_tile(g, t):
             words = kept["x", g][:, t, :].bitcast(F32)
-            h_t = psum.tile([P, PASSES, 2, P], F32, tag="turn", bufs=2)
+            lent = g == 0 and t % 2 == 1
+            h_t = psum.tile([P, PASSES, 2, P], F32, tag="act_t" if lent else "turn", bufs=2)
             for c in range(PASSES):
                 for u in range(2):
                     nc.tensor.transpose(h_t[:, c, u, :], words[:, 256 * c + u : 256 * (c + 1) : 2], ident[:])
@@ -168,7 +169,7 @@ def tile_stackrnn_pb_t_kernel(
             )
 
         def logits(g):
-            for j in range(ACTIONS + 1):
+            for j in (1, 0, 2, 3):
                 acc = psum.tile([P, GROUP], F32, tag="logit%d" % j)
                 cols = slice(j * S, (j + 1) * S)
                 for c in range(PASSES):
@@ -223,7 +224,8 @@ def tile_stackrnn_pb_t_kernel(
 
         def exp_of_shifted(g):
             e = work.tile([P, ACTIONS, GROUP], F32)
-            nc.scalar.activation(out=e[:], in_=kept["z", g][:], func=ACT.Exp)
+            for i in range(ACTIONS):
+                nc.scalar.activation(out=e[:, i, :], in_=kept["z", g][:, i, :], func=ACT.Exp)
             kept["e", g] = e
 
         def sum_first_two(g):
@@ -282,13 +284,16 @@ def tile_stackrnn_pb_t_kernel(
             nc.vector.tensor_tensor(out=pushed[:], in0=st[:, 0 : DEPTH - 1, :], in1=over_depth(0, DEPTH - 1), op=ALU.mult)
             popped = small.tile([P, DEPTH - 1, S], F32)
             nc.vector.tensor_tensor(out=popped[:], in0=st[:, 1:DEPTH, :], in1=over_depth(1, DEPTH - 1), op=ALU.mult)
+            if vector_adds(g, t):
+                nc.vector.tensor_tensor(out=new[:, 1:DEPTH, :], in0=new[:, 1:DEPTH, :], in1=pushed[:], op=ALU.add)
             nc.vector.scalar_tensor_tensor(
                 out=new[:, 0, :], in0=act_t[:, ACTIONS, :], scalar=0.5, in1=new[:, 0, :], op0=ALU.mult, op1=ALU.add
             )
             nc.vector.tensor_tensor(out=new[:, DEPTH - 1, :], in0=new[:, DEPTH - 1, :], in1=act_t[:, 1, :], op=ALU.subtract)
-            adder = nc.vector if vector_adds(g, t) else nc.gpsimd
-            adder.tensor_tensor(out=new[:, 1:DEPTH, :], in0=new[:, 1:DEPTH, :], in1=pushed[:], op=ALU.add)
-            nc.gpsimd.tensor_tensor(out=new[:, 0 : DEPTH - 1, :], in0=new[:, 0 : DEPTH - 1, :], in1=popped[:], op=ALU.add)
+            if not vector_adds(g, t):
+                nc.gpsimd.tensor_tensor(out=new[:, 1:DEPTH, :], in0=new[:, 1:DEPTH, :], in1=pushed[:], op=ALU.add)
+            adder = nc.vector if vector_adds(g, t) and t == TILES - 1 else nc.gpsimd
+            adder.tensor_tensor(out=new[:, 0 : DEPTH - 1, :], in0=new[:, 0 : DEPTH - 1, :], in1=popped[:], op=ALU.add)
             nc.sync.dma_start(out=out_1[group_rows(g)].rearrange("(p t) d s -> p t d s", t=TILES)[:, t, :, :], in_=new)
 
         def live(g):
@@ -340,8 +345,8 @@ def tile_stackrnn_pb_t_kernel(
             stage(r, transpose_weights, 1)
             stage(r + 1, sum_first_two)
             stage(r + 1, out_bias, 2)
-            stage(r + 2, quantise_h)
             stage(r + 1, log_of_sum)
+            stage(r + 2, quantise_h)
             stage(r + 1, out_bias, 3)
             stage(r + 1, store_out)
             stage(r + 3, new_quantise_input)

@@ -27,12 +27,9 @@ WA_COL = 0
 WS_COL = WA_COL + ACTIONS * S
 WO_COL = WS_COL + S
 W_COLS = WO_COL + ODIM
+STACK_BUFS = 3
 
 FLOPS = 2 * ROWS * K * W_COLS
-
-
-def vector_adds(g, t):
-    return g == GROUPS - 1
 
 
 def tile_stackrnn_pb_t_kernel(
@@ -59,10 +56,12 @@ def tile_stackrnn_pb_t_kernel(
                 nc.sync.dma_start(out=x[:, t, :], in_=rows[:, t, :])
             kept["x", g] = x
 
+        stack_tiles = [const.tile([P, TILES, DEPTH + 1, S], BF16, name="stack%d" % i) for i in range(STACK_BUFS)]
+
         def load_stack(g):
-            st = loads.tile([P, TILES, DEPTH, S], BF16)
+            st = stack_tiles[g % STACK_BUFS]
             nc.sync.dma_start(
-                out=st[:], in_=stack[group_rows(g)].rearrange("(p t) d s -> p t d s", t=TILES)
+                out=st[:, :, 0:DEPTH, :], in_=stack[group_rows(g)].rearrange("(p t) d s -> p t d s", t=TILES)
             )
             kept["st", g] = st
 
@@ -70,6 +69,12 @@ def tile_stackrnn_pb_t_kernel(
 
         ident = const.tile([P, P], F32)
         make_identity(nc, ident[:])
+        plus = const.tile([P, P], BF16)
+        nc.vector.tensor_copy(out=plus[:], in_=ident[:])
+        minus = const.tile([P, P], BF16)
+        nc.vector.tensor_scalar_mul(out=minus[:], in0=ident[:], scalar1=-1.0)
+        for st in stack_tiles:
+            nc.vector.memset(st[:, :, DEPTH, :], -1.0)
 
         w_words = const.tile([P, PASSES, W_COLS], U32, align_bytes=64)
         w_planes = const.tile([P, PASSES, W_COLS], U8, align_bytes=64)
@@ -100,15 +105,13 @@ def tile_stackrnn_pb_t_kernel(
         nc.scalar.dma_start(out=bias_rows[ACTIONS : ACTIONS + 1, :], in_=bs.rearrange("(a s) -> a s", a=1))
         bias_rows_f32 = const.tile([P, P], F32)
         bias_col = const.tile([P, ACTIONS + 1], F32)
-        half_bs = const.tile([P, 1], F32)
 
         def turn_biases():
             nc.vector.tensor_copy(out=bias_rows_f32[:], in_=bias_rows[:])
-            bias_t = psum.tile([P, ACTIONS + 1, P], F32, tag="act_t", bufs=2)
+            bias_t = psum.tile([P, ACTIONS + 1, P], F32, tag="planes", bufs=2)
             nc.tensor.transpose(bias_t[:, 0, :], bias_rows_f32[:], ident[:])
             nc.vector.tensor_copy(out=bias_col[:], in_=bias_t[:, 0, 0 : ACTIONS + 1])
-            nc.vector.tensor_scalar_mul(out=half_bs[:], in0=bias_t[:, 0, ACTIONS : ACTIONS + 1], scalar1=0.5)
-            bo_spread = psum.tile([P, ODIM], F32, tag="act_t", bufs=2)
+            bo_spread = psum.tile([P, ODIM], F32, tag="planes", bufs=2)
             nc.tensor.matmul(out=bo_spread[:], lhsT=ones[:], rhs=bo_alone[:], start=True, stop=True)
             nc.vector.tensor_copy(out=bo_rows[:], in_=bo_spread[:])
 
@@ -119,7 +122,7 @@ def tile_stackrnn_pb_t_kernel(
         def transpose_h_tile(g, t):
             words = kept["x", g][:, t, :].bitcast(F32)
             lent = g == 0 and t % 2 == 1
-            h_t = psum.tile([P, PASSES, 2, P], F32, tag="act_t" if lent else "turn", bufs=2)
+            h_t = psum.tile([P, PASSES, 2, P], F32, tag="planes" if lent else "quick", bufs=2)
             for c in range(PASSES):
                 for u in range(2):
                     nc.tensor.transpose(h_t[:, c, u, :], words[:, 256 * c + u : 256 * (c + 1) : 2], ident[:])
@@ -145,7 +148,7 @@ def tile_stackrnn_pb_t_kernel(
 
         def out_passes(g, t):
             rows = slice(t * P, (t + 1) * P)
-            acc = psum.tile([P, ODIM], F32, tag="turn", bufs=2)
+            acc = psum.tile([P, ODIM], F32, tag="out", bufs=1)
             for c in range(PASSES):
                 nc.tensor.matmul_mx(
                     out=acc[:],
@@ -168,132 +171,145 @@ def tile_stackrnn_pb_t_kernel(
                 out=out_0[group_rows(g), :].rearrange("(p t) n -> p t n", t=TILES), in_=kept["out_sb", g][:]
             )
 
-        def logits(g):
-            for j in (1, 0, 2, 3):
-                acc = psum.tile([P, GROUP], F32, tag="logit%d" % j)
-                cols = slice(j * S, (j + 1) * S)
-                for c in range(PASSES):
-                    nc.tensor.matmul_mx(
-                        out=acc[:],
-                        lhsT=w_words[:, c, cols].bitcast(FP8X4),
-                        lhsT_scale=w_planes[:, c, cols],
-                        rhs=kept["h_words", g][:, c, :].bitcast(FP8X4),
-                        rhs_scale=kept["h_planes", g][:, c, :],
-                        start=(c == 0),
-                        stop=(c == PASSES - 1),
-                    )
-                kept["logit%d" % j, g] = acc
-            pop_logit = work.tile([P, GROUP], F32)
+        def logit(g, j):
+            long_lived = j in (0, 1)
+            acc = psum.tile([P, GROUP], F32, tag="long" if long_lived else "quick", bufs=1 if long_lived else 2)
+            cols = slice(j * S, (j + 1) * S)
+            for c in range(PASSES):
+                nc.tensor.matmul_mx(
+                    out=acc[:],
+                    lhsT=w_words[:, c, cols].bitcast(FP8X4),
+                    lhsT_scale=w_planes[:, c, cols],
+                    rhs=kept["h_words", g][:, c, :].bitcast(FP8X4),
+                    rhs_scale=kept["h_planes", g][:, c, :],
+                    start=(c == 0),
+                    stop=(c == PASSES - 1),
+                )
+            kept["logit%d" % j, g] = acc
+
+        def new_planes(g):
+            planes = work.tile([P, 3, GROUP], F32, bufs=3)
+            kept["planes", g] = planes
+
+        def copy_noop(g):
+            noop = work.tile([P, GROUP], F32)
+            nc.scalar.activation(out=noop[:], in_=kept["logit2", g][:], func=ACT.Identity, bias=bias_col[:, 2:3], scale=1.0)
+            kept["noop", g] = noop
+
+        def top_of(g):
             nc.scalar.activation(
-                out=pop_logit[:], in_=kept["logit1", g][:], func=ACT.Identity, bias=bias_col[:, 1:2], scale=1.0
+                out=kept["planes", g][:, 2, :], in_=kept["logit3", g][:], func=ACT.Sigmoid, bias=bias_col[:, 3:4], scale=1.0
             )
-            kept["pop_logit", g] = pop_logit
 
-        def peak_first(g):
-            top2 = work.tile([P, GROUP], F32)
+        def gap_of(g):
+            gap = work.tile([P, GROUP], F32)
             nc.vector.scalar_tensor_tensor(
-                out=top2[:], in0=kept["logit0", g][:], scalar=bias_col[:, 0:1], in1=kept["pop_logit", g][:],
-                op0=ALU.add, op1=ALU.max,
+                out=gap[:], in0=kept["logit0", g][:], scalar=bias_col[:, 0:1], in1=kept["noop", g][:],
+                op0=ALU.add, op1=ALU.subtract,
             )
-            kept["top2", g] = top2
+            kept["gap", g] = gap
 
-        def peak_second(g):
+        def peak_of(g):
             peak = work.tile([P, GROUP], F32)
             nc.vector.scalar_tensor_tensor(
-                out=peak[:], in0=kept["logit2", g][:], scalar=bias_col[:, 2:3], in1=kept["top2", g][:],
+                out=peak[:], in0=kept["logit0", g][:], scalar=bias_col[:, 0:1], in1=kept["noop", g][:],
                 op0=ALU.add, op1=ALU.max,
             )
             kept["peak", g] = peak
 
-        def shifted_logits(g):
-            peak = kept["peak", g]
-            z = work.tile([P, ACTIONS, GROUP], F32)
-            for i in range(ACTIONS):
-                nc.vector.scalar_tensor_tensor(
-                    out=z[:, i, :], in0=kept["logit%d" % i, g][:], scalar=bias_col[:, i : i + 1], in1=peak[:],
-                    op0=ALU.add, op1=ALU.subtract,
-                )
-            kept["z", g] = z
-
-        def tanh_of_top(g):
-            tanh_half = work.tile([P, GROUP], F32)
-            nc.scalar.activation(
-                out=tanh_half[:], in_=kept["logit3", g][:], func=ACT.Tanh, bias=half_bs[:, 0:1], scale=0.5
-            )
-            kept["tanh_half", g] = tanh_half
-
-        def exp_of_shifted(g):
-            e = work.tile([P, ACTIONS, GROUP], F32)
-            for i in range(ACTIONS):
-                nc.scalar.activation(out=e[:, i, :], in_=kept["z", g][:, i, :], func=ACT.Exp)
-            kept["e", g] = e
-
-        def sum_first_two(g):
-            e = kept["e", g]
-            e01 = work.tile([P, GROUP], F32)
-            nc.vector.tensor_tensor(out=e01[:], in0=e[:, 0, :], in1=e[:, 1, :], op=ALU.add)
-            kept["e01", g] = e01
-
-        def log_of_sum(g):
-            total = work.tile([P, GROUP], F32)
-            nc.vector.tensor_tensor(out=total[:], in0=kept["e01", g][:], in1=kept["e", g][:, 2, :], op=ALU.add)
-            log_total = work.tile([P, GROUP], F32)
-            nc.scalar.activation(out=log_total[:], in_=total[:], func=ACT.Ln)
-            kept["log_total", g] = log_total
-
-        def log_weights(g):
-            log_act = work.tile([P, ACTIONS, GROUP], F32)
-            nc.gpsimd.tensor_tensor(
-                out=log_act[:], in0=kept["z", g][:],
-                in1=kept["log_total", g][:].unsqueeze(1).to_broadcast([P, ACTIONS, GROUP]), op=ALU.subtract,
-            )
-            kept["log_act", g] = log_act
-
-        def weights(g):
-            act = work.tile([P, ACTIONS + 1, GROUP], F32)
-            nc.scalar.activation(out=act[:, 0:ACTIONS, :], in_=kept["log_act", g][:], func=ACT.Exp)
-            kept["act", g] = act
-
-        def push_of_top(g):
-            act = kept["act", g]
+        def pop_less_peak(g):
+            below = work.tile([P, GROUP], F32)
             nc.vector.scalar_tensor_tensor(
-                out=act[:, ACTIONS, :], in0=kept["tanh_half", g][:], scalar=1.0, in1=act[:, 0, :],
-                op0=ALU.add, op1=ALU.mult,
+                out=below[:], in0=kept["logit1", g][:], scalar=bias_col[:, 1:2], in1=kept["peak", g][:],
+                op0=ALU.add, op1=ALU.subtract,
             )
+            kept["below", g] = below
+
+        def share_of_push(g):
+            nc.scalar.activation(out=kept["planes", g][:, 0, :], in_=kept["gap", g][:], func=ACT.Sigmoid)
+
+        def larger_share(g):
+            off_half = work.tile([P, GROUP], F32)
+            nc.scalar.activation(out=off_half[:], in_=kept["planes", g][:, 0, :], func=ACT.Abs, bias=-0.5, scale=1.0)
+            kept["off_half", g] = off_half
+
+        def log_of_larger_share(g):
+            log_share = work.tile([P, GROUP], F32)
+            nc.scalar.activation(out=log_share[:], in_=kept["off_half", g][:], func=ACT.Ln, bias=0.5, scale=1.0)
+            kept["log_share", g] = log_share
+
+        def pop_less_both(g):
+            odds = work.tile([P, GROUP], F32)
+            nc.gpsimd.tensor_tensor(out=odds[:], in0=kept["below", g][:], in1=kept["log_share", g][:], op=ALU.add)
+            kept["odds", g] = odds
+
+        def share_of_both(g):
+            nc.scalar.activation(out=kept["planes", g][:, 1, :], in_=kept["odds", g][:], func=ACT.Sigmoid, scale=-1.0)
 
         def new_stack_tile(g):
             new_sb = work.tile([P, TILES, DEPTH, S], F32)
             kept["new_sb", g] = new_sb
 
-        def transpose_weights(g, t):
-            act_t = psum.tile([P, ACTIONS + 1, P], F32, tag="act_t", bufs=2)
-            for j in range(ACTIONS + 1):
-                nc.tensor.transpose(act_t[:, j, :], kept["act", g][:, j, t * P : (t + 1) * P], ident[:])
-            kept["act_t", g, t] = act_t
+        def turn_planes(g, t):
+            planes_t = psum.tile([P, 3, P], F32, tag="planes", bufs=2)
+            for j in range(3):
+                nc.tensor.transpose(planes_t[:, j, :], kept["planes", g][:, j, t * P : (t + 1) * P], ident[:])
+            kept["planes_t", g, t] = planes_t
 
-        def blend_tile(g, t):
-            st = kept["st", g][:, t, :, :]
-            new = kept["new_sb", g][:, t, :, :]
-            act_t = kept["act_t", g, t]
+        def turn_shares(g):
+            shares_t = psum.tile([P, TILES, P], F32, tag="quick", bufs=2)
+            for t in range(TILES):
+                nc.tensor.transpose(shares_t[:, t, :], kept["planes", g][:, 0, t * P : (t + 1) * P], ident[:])
+            p_sb = work.tile([P, TILES, S], F32, bufs=3)
+            nc.scalar.copy(out=p_sb[:], in_=shares_t[:])
+            kept["p_sb", g] = p_sb
 
-            def over_depth(j, depth):
-                return act_t[:, j, :].unsqueeze(1).to_broadcast([P, depth, S])
+        def steps_of_stack(g, t):
+            st = kept["st", g]
+            steps = psum.tile([P, DEPTH - 1, S], F32, tag="steps", bufs=2)
+            nc.tensor.matmul(out=steps[:], lhsT=plus[:], rhs=st[:, t, 0 : DEPTH - 1, :], start=True, stop=False)
+            nc.tensor.matmul(out=steps[:], lhsT=minus[:], rhs=st[:, t, 1:DEPTH, :], start=False, stop=True)
+            kept["steps", g, t] = steps
 
-            nc.vector.tensor_tensor(out=new, in0=st, in1=over_depth(2, DEPTH), op=ALU.mult)
-            pushed = small.tile([P, DEPTH - 1, S], F32)
-            nc.vector.tensor_tensor(out=pushed[:], in0=st[:, 0 : DEPTH - 1, :], in1=over_depth(0, DEPTH - 1), op=ALU.mult)
-            popped = small.tile([P, DEPTH - 1, S], F32)
-            nc.vector.tensor_tensor(out=popped[:], in0=st[:, 1:DEPTH, :], in1=over_depth(1, DEPTH - 1), op=ALU.mult)
-            if vector_adds(g, t):
-                nc.vector.tensor_tensor(out=new[:, 1:DEPTH, :], in0=new[:, 1:DEPTH, :], in1=pushed[:], op=ALU.add)
-            nc.vector.scalar_tensor_tensor(
-                out=new[:, 0, :], in0=act_t[:, ACTIONS, :], scalar=0.5, in1=new[:, 0, :], op0=ALU.mult, op1=ALU.add
+        def blend_a(g, t):
+            first = small.tile([P, S], F32)
+            nc.vector.tensor_tensor(out=first[:], in0=kept["planes_t", g, t][:, 2, :], in1=kept["st", g][:, t, 0, :], op=ALU.subtract)
+            kept["first", g, t] = first
+            scaled = small.tile([P, DEPTH, S], F32)
+            kept["scaled", g, t] = scaled
+            inner = small.tile([P, DEPTH, S], F32)
+            kept["inner", g, t] = inner
+
+        def blend_b(g, t):
+            nc.vector.tensor_tensor(out=kept["scaled", g, t][:, 0, :], in0=kept["planes_t", g, t][:, 0, :], in1=kept["first", g, t][:], op=ALU.mult)
+
+        def blend_c(g, t):
+            nc.vector.tensor_tensor(
+                out=kept["scaled", g, t][:, 1:DEPTH, :], in0=kept["steps", g, t][:],
+                in1=kept["p_sb", g][:, t, :].unsqueeze(1).to_broadcast([P, DEPTH - 1, S]), op=ALU.mult,
             )
-            nc.vector.tensor_tensor(out=new[:, DEPTH - 1, :], in0=new[:, DEPTH - 1, :], in1=act_t[:, 1, :], op=ALU.subtract)
-            if not vector_adds(g, t):
-                nc.gpsimd.tensor_tensor(out=new[:, 1:DEPTH, :], in0=new[:, 1:DEPTH, :], in1=pushed[:], op=ALU.add)
-            adder = nc.vector if vector_adds(g, t) and t == TILES - 1 else nc.gpsimd
-            adder.tensor_tensor(out=new[:, 0 : DEPTH - 1, :], in0=new[:, 0 : DEPTH - 1, :], in1=popped[:], op=ALU.add)
+
+        def blend_d(g, t):
+            nc.vector.tensor_tensor(
+                out=kept["inner", g, t][:, 0 : DEPTH - 1, :], in0=kept["steps", g, t][:], in1=kept["scaled", g, t][:, 0 : DEPTH - 1, :], op=ALU.add
+            )
+
+        def blend_e(g, t):
+            nc.vector.scalar_tensor_tensor(
+                out=kept["inner", g, t][:, DEPTH - 1, :], in0=kept["st", g][:, t, DEPTH - 1, :], scalar=1.0,
+                in1=kept["scaled", g, t][:, DEPTH - 1, :], op0=ALU.add, op1=ALU.add,
+            )
+
+        def blend_f(g, t):
+            moved = small.tile([P, DEPTH, S], F32)
+            nc.vector.tensor_tensor(
+                out=moved[:], in0=kept["planes_t", g, t][:, 1, :].unsqueeze(1).to_broadcast([P, DEPTH, S]), in1=kept["inner", g, t][:], op=ALU.mult
+            )
+            kept["moved", g, t] = moved
+
+        def blend_g(g, t):
+            new = kept["new_sb", g][:, t, :, :]
+            nc.gpsimd.tensor_tensor(out=new, in0=kept["moved", g, t][:], in1=kept["st", g][:, t, 1 : DEPTH + 1, :], op=ALU.add)
             nc.sync.dma_start(out=out_1[group_rows(g)].rearrange("(p t) d s -> p t d s", t=TILES)[:, t, :, :], in_=new)
 
         def live(g):
@@ -303,51 +319,90 @@ def tile_stackrnn_pb_t_kernel(
             if live(g):
                 step(g, *args)
 
+        AHEAD = 5
+
+        def front_prepare(f):
+            g, t = f // TILES, f % TILES
+            if t == 0:
+                stage(g, new_out_tile)
+            stage(g, out_passes, t)
+
+        def blend_prepare(k):
+            g, t = k // TILES, k % TILES
+            if t == 0:
+                stage(g, new_stack_tile)
+            stage(g, steps_of_stack, t)
+            stage(g, turn_planes, t)
+
         load_h(1)
         new_quantise_input(0)
         for t in range(TILES):
             transpose_h_tile(0, t)
+        turn_biases()
         load_h(2)
         quantise_h(0)
         new_quantise_input(1)
+        load_stack(0)
+        load_stack(1)
+        new_planes(0)
+        logit(0, 2)
+        logit(0, 0)
+        copy_noop(0)
         transpose_h_tile(1, 0)
-        turn_biases()
-        for r in range(-1, GROUPS + 1):
-            stage(r + 4, load_h)
-            stage(r + 1, load_stack)
-            stage(r, log_weights)
-            stage(r - 1, new_stack_tile)
-            stage(r + 1, logits)
-            stage(r + 1, new_out_tile)
-            stage(r + 1, out_passes, 0)
-            stage(r + 1, tanh_of_top)
-            stage(r - 1, blend_tile, 0)
-            stage(r - 1, transpose_weights, 2)
-            stage(r + 2, transpose_h_tile, 1)
-            stage(r - 1, blend_tile, 1)
-            stage(r - 1, transpose_weights, 3)
-            stage(r, weights)
-            stage(r + 1, peak_first)
-            stage(r + 1, out_bias, 0)
-            stage(r + 2, transpose_h_tile, 2)
-            stage(r + 1, out_passes, 1)
-            stage(r + 1, peak_second)
-            stage(r - 1, blend_tile, 2)
-            stage(r + 1, shifted_logits)
-            stage(r + 1, exp_of_shifted)
-            stage(r + 2, transpose_h_tile, 3)
-            stage(r + 1, out_bias, 1)
-            stage(r + 1, out_passes, 2)
-            stage(r - 1, blend_tile, 3)
-            stage(r + 1, out_passes, 3)
-            stage(r, push_of_top)
-            stage(r, transpose_weights, 0)
-            stage(r, transpose_weights, 1)
-            stage(r + 1, sum_first_two)
-            stage(r + 1, out_bias, 2)
-            stage(r + 1, log_of_sum)
-            stage(r + 2, quantise_h)
-            stage(r + 1, out_bias, 3)
-            stage(r + 1, store_out)
-            stage(r + 3, new_quantise_input)
-            stage(r + 3, transpose_h_tile, 0)
+        logit(0, 3)
+        top_of(0)
+        front_prepare(0)
+        transpose_h_tile(1, 1)
+        transpose_h_tile(1, 2)
+        gap_of(0)
+        share_of_push(0)
+        larger_share(0)
+        for k in range(-AHEAD, GROUPS * TILES):
+            f = k + AHEAD
+            b, t = k // TILES, k % TILES
+            m, u = f // TILES, f % TILES
+            if u == 0:
+                stage(m + 3, load_h)
+            if t == 0:
+                stage(b + 2, load_stack)
+            blend_prepare(k + 1)
+            if u == 0:
+                stage(m + 1, transpose_h_tile, 3)
+                stage(m, log_of_larger_share)
+            if u == 1:
+                stage(m, logit, 1)
+                stage(m + 2, new_quantise_input)
+                stage(m + 2, transpose_h_tile, 0)
+                stage(m, turn_shares)
+            if u == 2:
+                stage(m + 2, transpose_h_tile, 1)
+                stage(m + 1, new_planes)
+                stage(m + 1, logit, 2)
+                stage(m + 1, logit, 0)
+                stage(m + 1, copy_noop)
+            if u == 3:
+                stage(m, share_of_both)
+                stage(m + 1, logit, 3)
+                stage(m + 1, top_of)
+                stage(m + 2, transpose_h_tile, 2)
+            stage(b, blend_a, t)
+            stage(b, blend_c, t)
+            stage(b, blend_b, t)
+            stage(m, out_bias, u)
+            front_prepare(f + 1)
+            stage(b, blend_d, t)
+            stage(b, blend_e, t)
+            if u == 0:
+                stage(m, peak_of)
+            if u == 1:
+                stage(m + 1, quantise_h)
+            if u == 2:
+                stage(m, pop_less_peak)
+                stage(m, pop_less_both)
+            if u == 3:
+                stage(m, store_out)
+                stage(m + 1, gap_of)
+                stage(m + 1, share_of_push)
+                stage(m + 1, larger_share)
+            stage(b, blend_f, t)
+            stage(b, blend_g, t)

@@ -106,29 +106,39 @@ def tile_stackrnn_pb_t_kernel(
         bias_rows_f32 = const.tile([P, P], F32)
         bias_col = const.tile([P, ACTIONS + 1], F32)
 
-        def turn_biases():
+        def widen_biases():
             nc.vector.tensor_copy(out=bias_rows_f32[:], in_=bias_rows[:])
-            bias_t = psum.tile([P, ACTIONS + 1, P], F32, tag="planes", bufs=2)
+
+        def turn_biases():
+            bias_t = psum.tile([P, ACTIONS + 1, P], F32, tag="steps", bufs=2)
             nc.tensor.transpose(bias_t[:, 0, :], bias_rows_f32[:], ident[:])
-            nc.vector.tensor_copy(out=bias_col[:], in_=bias_t[:, 0, 0 : ACTIONS + 1])
-            bo_spread = psum.tile([P, ODIM], F32, tag="planes", bufs=2)
+            bo_spread = psum.tile([P, ODIM], F32, tag="steps", bufs=2)
             nc.tensor.matmul(out=bo_spread[:], lhsT=ones[:], rhs=bo_alone[:], start=True, stop=True)
-            nc.vector.tensor_copy(out=bo_rows[:], in_=bo_spread[:])
+            kept["bias_t"] = bias_t
+            kept["bo_spread"] = bo_spread
+
+        def keep_biases():
+            nc.vector.tensor_copy(out=bias_col[:], in_=kept["bias_t"][:, 0, 0 : ACTIONS + 1])
+            nc.vector.tensor_copy(out=bo_rows[:], in_=kept["bo_spread"][:])
 
         def new_quantise_input(g):
             grouped = work.tile([P, PASSES, TILES, P, 4], BF16, align_bytes=64)
             kept["grouped", g] = grouped
 
-        def transpose_h_tile(g, t):
+        def transpose_h_tile(g, t, bank="quick", copier=nc.scalar.copy):
             words = kept["x", g][:, t, :].bitcast(F32)
-            lent = g == 0 and t % 2 == 1
-            h_t = psum.tile([P, PASSES, 2, P], F32, tag="planes" if lent else "quick", bufs=2)
+            h_t = psum.tile([P, PASSES, 2, P], F32, tag=bank, bufs=2)
             for c in range(PASSES):
                 for u in range(2):
                     nc.tensor.transpose(h_t[:, c, u, :], words[:, 256 * c + u : 256 * (c + 1) : 2], ident[:])
-            nc.scalar.copy(
+            kept["h_t", g, t] = h_t
+            if copier is not None:
+                keep_h_tile(g, t, copier)
+
+        def keep_h_tile(g, t, copier):
+            copier(
                 out=kept["grouped", g][:].bitcast(F32)[:, :, t, :, :],
-                in_=h_t[:].rearrange("p c u r -> p c r u"),
+                in_=kept["h_t", g, t][:].rearrange("p c u r -> p c r u"),
             )
 
         def quantise_h(g):
@@ -141,6 +151,26 @@ def tile_stackrnn_pb_t_kernel(
             )
             kept["h_words", g] = h_words
             kept["h_planes", g] = h_planes
+
+        def quantise_h_by_tiles(g):
+            h_words = work.tile([P, PASSES, GROUP], U32, align_bytes=64)
+            h_planes = work.tile([P, PASSES, GROUP], U8, align_bytes=64)
+            kept["h_words", g] = h_words
+            kept["h_planes", g] = h_planes
+
+        def quantise_h_tile(g, t):
+            rows = slice(t * P, (t + 1) * P)
+            for c in range(PASSES):
+                nc.vector.quantize_mx(
+                    out=kept["h_words", g][:, c, rows].bitcast(FP8X4),
+                    scales=kept["h_planes", g][:, c, rows],
+                    in_=kept["grouped", g][:, c, t, :, :].rearrange("p r j -> p (r j)"),
+                )
+
+        scrap = const.tile([P, 1], F32)
+
+        def load_sigmoid_table():
+            nc.scalar.activation(out=scrap[:], in_=ident[:, 0:1], func=ACT.Sigmoid)
 
         def new_out_tile(g):
             out_sb = work.tile([P, TILES, ODIM], F32)
@@ -251,17 +281,25 @@ def tile_stackrnn_pb_t_kernel(
             kept["new_sb", g] = new_sb
 
         def turn_planes(g, t):
-            planes_t = psum.tile([P, 3, P], F32, tag="planes", bufs=2)
+            if t == 0:
+                new_stack_tile(g)
+            lent = TILES * g + t in (GROUPS * TILES - 4, GROUPS * TILES - 3)
+            planes_t = psum.tile([P, 3, P], F32, tag="quick" if lent else "planes", bufs=2)
             for j in range(3):
                 nc.tensor.transpose(planes_t[:, j, :], kept["planes", g][:, j, t * P : (t + 1) * P], ident[:])
             kept["planes_t", g, t] = planes_t
 
-        def turn_shares(g):
+        def turn_shares(g, copier=nc.scalar.copy):
             shares_t = psum.tile([P, TILES, P], F32, tag="quick", bufs=2)
             for t in range(TILES):
                 nc.tensor.transpose(shares_t[:, t, :], kept["planes", g][:, 0, t * P : (t + 1) * P], ident[:])
+            kept["shares_t", g] = shares_t
+            if copier is not None:
+                keep_shares(g, copier)
+
+        def keep_shares(g, copier):
             p_sb = work.tile([P, TILES, S], F32, bufs=3)
-            nc.scalar.copy(out=p_sb[:], in_=shares_t[:])
+            copier(out=p_sb[:], in_=kept["shares_t", g][:])
             kept["p_sb", g] = p_sb
 
         def steps_of_stack(g, t):
@@ -319,90 +357,167 @@ def tile_stackrnn_pb_t_kernel(
             if live(g):
                 step(g, *args)
 
-        AHEAD = 5
+        done = set()
+        LAST = GROUPS * TILES - 1
+
+        def once(g, step, *args):
+            if live(g) and (step, g, args) not in done:
+                done.add((step, g, args))
+                step(g, *args)
+
+        def tile_stage(k, step):
+            stage(k // TILES, step, k % TILES)
 
         def front_prepare(f):
             g, t = f // TILES, f % TILES
             if t == 0:
-                stage(g, new_out_tile)
-            stage(g, out_passes, t)
+                once(g, new_out_tile)
+            once(g, out_passes, t)
 
-        def blend_prepare(k):
-            g, t = k // TILES, k % TILES
-            if t == 0:
-                stage(g, new_stack_tile)
-            stage(g, steps_of_stack, t)
-            stage(g, turn_planes, t)
-
-        load_h(1)
-        new_quantise_input(0)
-        for t in range(TILES):
-            transpose_h_tile(0, t)
-        turn_biases()
-        load_h(2)
-        quantise_h(0)
-        new_quantise_input(1)
-        load_stack(0)
-        load_stack(1)
-        new_planes(0)
-        logit(0, 2)
-        logit(0, 0)
-        copy_noop(0)
-        transpose_h_tile(1, 0)
-        logit(0, 3)
-        top_of(0)
-        front_prepare(0)
-        transpose_h_tile(1, 1)
-        transpose_h_tile(1, 2)
-        gap_of(0)
-        share_of_push(0)
-        larger_share(0)
-        for k in range(-AHEAD, GROUPS * TILES):
-            f = k + AHEAD
-            b, t = k // TILES, k % TILES
+        def front_issue(f):
             m, u = f // TILES, f % TILES
             if u == 0:
-                stage(m + 3, load_h)
-            if t == 0:
-                stage(b + 2, load_stack)
-            blend_prepare(k + 1)
-            if u == 0:
-                stage(m + 1, transpose_h_tile, 3)
-                stage(m, log_of_larger_share)
+                once(m + 3, load_h)
+                once(m + 1, transpose_h_tile, 3)
+                once(m, log_of_larger_share)
             if u == 1:
-                stage(m, logit, 1)
-                stage(m + 2, new_quantise_input)
-                stage(m + 2, transpose_h_tile, 0)
-                stage(m, turn_shares)
+                once(m, logit, 1)
+                once(m + 2, new_quantise_input)
+                once(m + 2, transpose_h_tile, 0)
+                once(m, turn_shares)
             if u == 2:
-                stage(m + 2, transpose_h_tile, 1)
-                stage(m + 1, new_planes)
-                stage(m + 1, logit, 2)
-                stage(m + 1, logit, 0)
-                stage(m + 1, copy_noop)
+                once(m + 2, transpose_h_tile, 1)
             if u == 3:
-                stage(m, share_of_both)
-                stage(m + 1, logit, 3)
-                stage(m + 1, top_of)
-                stage(m + 2, transpose_h_tile, 2)
-            stage(b, blend_a, t)
-            stage(b, blend_c, t)
-            stage(b, blend_b, t)
-            stage(m, out_bias, u)
+                once(m, share_of_both)
+                once(m + 1, logit, 3)
+                once(m + 1, top_of)
+                once(m + 2, transpose_h_tile, 2)
+
+        def front_out(f):
+            once(f // TILES, out_bias, f % TILES)
             front_prepare(f + 1)
-            stage(b, blend_d, t)
-            stage(b, blend_e, t)
-            if u == 0:
-                stage(m, peak_of)
-            if u == 1:
-                stage(m + 1, quantise_h)
-            if u == 2:
-                stage(m, pop_less_peak)
-                stage(m, pop_less_both)
-            if u == 3:
-                stage(m, store_out)
-                stage(m + 1, gap_of)
-                stage(m + 1, share_of_push)
-                stage(m + 1, larger_share)
-            stage(b, blend_f, t)
-            stage(b, blend_g, t)
+
+        def front_fill(f, early):
+            m, u = f // TILES, f % TILES
+            if u == 0 and not early:
+                once(m, peak_of)
+            if u == 1 and early:
+                once(m + 1, quantise_h)
+            if u == 2 and early:
+                once(m, pop_less_peak)
+                once(m, pop_less_both)
+                once(m + 1, new_planes)
+                once(m + 1, logit, 2)
+                once(m + 1, logit, 0)
+                once(m + 1, copy_noop)
+            if u == 3 and not early:
+                once(m, store_out)
+                once(m + 1, gap_of)
+                once(m + 1, share_of_push)
+                once(m + 1, larger_share)
+
+        TAIL = LAST - 5
+
+        def planes_due(k):
+            if k < TAIL:
+                return (k + 1,)
+            if k == TAIL:
+                return (k + 1, k + 2)
+            return (k + 2,)
+
+        def begin_tile(k):
+            tile_stage(k, blend_a)
+            tile_stage(k, blend_c)
+            tile_stage(k, blend_b)
+
+        def slot(k, steps):
+            if k % TILES == 0:
+                once(k // TILES + 2, load_stack)
+            front_issue(steps[0])
+            for ahead in planes_due(k):
+                tile_stage(ahead, turn_planes)
+            tile_stage(k, blend_e)
+            front_fill(steps[0], True)
+            front_out(steps[0])
+            tile_stage(k, blend_d)
+            tile_stage(k + 2, steps_of_stack)
+            front_fill(steps[0], False)
+            begin_tile(k + 1)
+            tile_stage(k, blend_f)
+            tile_stage(k, blend_g)
+            for f in steps[1:]:
+                front_issue(f)
+                front_fill(f, True)
+                front_out(f)
+                front_fill(f, False)
+
+        by_vector = nc.vector.tensor_copy
+
+        def ahead_of_turn(step, g, *args, **how):
+            done.add((step, g, args))
+            step(g, *args, **how)
+
+        load_sigmoid_table()
+        once(1, load_h)
+        once(0, new_quantise_input)
+        quantise_h_by_tiles(0)
+        done.add((quantise_h, 0, ()))
+        for t in range(TILES):
+            transpose_h_tile(0, t, "planes" if t % 2 else "quick")
+            quantise_h_tile(0, t)
+            if t == 0:
+                widen_biases()
+        once(2, load_h)
+        once(0, load_stack)
+        once(1, load_stack)
+        once(3, load_h)
+        turn_biases()
+        keep_biases()
+        once(0, new_planes)
+        once(1, new_quantise_input)
+        once(0, logit, 2)
+        once(0, logit, 0)
+        once(0, copy_noop)
+        once(0, logit, 3)
+        front_prepare(0)
+        ahead_of_turn(transpose_h_tile, 1, 0, bank="planes", copier=None)
+        ahead_of_turn(transpose_h_tile, 1, 1, bank="planes", copier=None)
+        once(0, gap_of)
+        once(0, peak_of)
+        once(0, share_of_push)
+        once(0, larger_share)
+        once(0, logit, 1)
+        ahead_of_turn(turn_shares, 0, copier=None)
+        front_out(0)
+        keep_h_tile(1, 0, by_vector)
+        keep_h_tile(1, 1, by_vector)
+        ahead_of_turn(transpose_h_tile, 1, 2, bank="steps", copier=None)
+        ahead_of_turn(transpose_h_tile, 1, 3, bank="steps", copier=None)
+        once(0, log_of_larger_share)
+        once(0, pop_less_peak)
+        once(0, pop_less_both)
+        once(0, top_of)
+        keep_shares(0, by_vector)
+        front_out(1)
+        keep_h_tile(1, 2, by_vector)
+        keep_h_tile(1, 3, by_vector)
+        once(0, share_of_both)
+        once(1, quantise_h)
+        turn_planes(0, 0)
+        steps_of_stack(0, 0)
+        steps_of_stack(0, 1)
+        front_out(2)
+        once(1, new_planes)
+        once(1, logit, 2)
+        once(1, logit, 0)
+        once(1, copy_noop)
+        once(2, new_quantise_input)
+        once(2, transpose_h_tile, 0)
+        begin_tile(0)
+        once(2, transpose_h_tile, 1)
+        slot(0, (3,))
+        slot(1, (4, 5))
+        slot(2, (6,))
+        slot(3, (7, 8))
+        for k in range(4, GROUPS * TILES):
+            slot(k, (k + 5,))

@@ -127,7 +127,7 @@ def tile_stackrnn_pb_t_kernel(
 
         def transpose_h_tile(g, t, bank="quick", copier=nc.scalar.copy):
             words = kept["x", g][:, t, :].bitcast(F32)
-            h_t = psum.tile([P, PASSES, 2, P], F32, tag=bank, bufs=2)
+            h_t = psum.tile([P, PASSES, 2, P], F32, tag=bank, bufs=1 if bank == "long" else 2)
             for c in range(PASSES):
                 for u in range(2):
                     nc.tensor.transpose(h_t[:, c, u, :], words[:, 256 * c + u : 256 * (c + 1) : 2], ident[:])
@@ -297,6 +297,14 @@ def tile_stackrnn_pb_t_kernel(
             if copier is not None:
                 keep_shares(g, copier)
 
+        def turn_sums(g):
+            sums_t = psum.tile([P, TILES, P], F32, tag="quick", bufs=2)
+            for t in range(TILES):
+                nc.tensor.transpose(sums_t[:, t, :], kept["planes", g][:, 1, t * P : (t + 1) * P], ident[:])
+            q_sb = work.tile([P, TILES, S], F32, bufs=3)
+            nc.scalar.copy(out=q_sb[:], in_=sums_t[:])
+            kept["q_sb", g] = q_sb
+
         def keep_shares(g, copier):
             p_sb = work.tile([P, TILES, S], F32, bufs=3)
             copier(out=p_sb[:], in_=kept["shares_t", g][:])
@@ -338,12 +346,20 @@ def tile_stackrnn_pb_t_kernel(
                 in1=kept["scaled", g, t][:, DEPTH - 1, :], op0=ALU.add, op1=ALU.add,
             )
 
-        def blend_f(g, t):
+        def blend_f_low(g, t, own):
             moved = small.tile([P, DEPTH, S], F32)
-            nc.vector.tensor_tensor(
-                out=moved[:], in0=kept["planes_t", g, t][:, 1, :].unsqueeze(1).to_broadcast([P, DEPTH, S]), in1=kept["inner", g, t][:], op=ALU.mult
-            )
             kept["moved", g, t] = moved
+            if own < DEPTH:
+                nc.gpsimd.tensor_tensor(
+                    out=moved[:, own:DEPTH, :], in0=kept["inner", g, t][:, own:DEPTH, :],
+                    in1=kept["q_sb", g][:, t, :].unsqueeze(1).to_broadcast([P, DEPTH - own, S]), op=ALU.mult,
+                )
+
+        def blend_f(g, t, own):
+            nc.vector.tensor_tensor(
+                out=kept["moved", g, t][:, 0:own, :], in0=kept["planes_t", g, t][:, 1, :].unsqueeze(1).to_broadcast([P, own, S]),
+                in1=kept["inner", g, t][:, 0:own, :], op=ALU.mult,
+            )
 
         def blend_g(g, t):
             new = kept["new_sb", g][:, t, :, :]
@@ -359,6 +375,9 @@ def tile_stackrnn_pb_t_kernel(
 
         done = set()
         LAST = GROUPS * TILES - 1
+        OUT_AHEAD = 3
+        CHAIN_AHEAD = 2
+        TAIL = LAST - 3 - CHAIN_AHEAD
 
         def once(g, step, *args):
             if live(g) and (step, g, args) not in done:
@@ -374,49 +393,11 @@ def tile_stackrnn_pb_t_kernel(
                 once(g, new_out_tile)
             once(g, out_passes, t)
 
-        def front_issue(f):
-            m, u = f // TILES, f % TILES
-            if u == 0:
-                once(m + 3, load_h)
-                once(m + 1, transpose_h_tile, 3)
-                once(m, log_of_larger_share)
-            if u == 1:
-                once(m, logit, 1)
-                once(m + 2, new_quantise_input)
-                once(m + 2, transpose_h_tile, 0)
-                once(m, turn_shares)
-            if u == 2:
-                once(m + 2, transpose_h_tile, 1)
-            if u == 3:
-                once(m, share_of_both)
-                once(m + 1, logit, 3)
-                once(m + 1, top_of)
-                once(m + 2, transpose_h_tile, 2)
-
         def front_out(f):
             once(f // TILES, out_bias, f % TILES)
             front_prepare(f + 1)
-
-        def front_fill(f, early):
-            m, u = f // TILES, f % TILES
-            if u == 0 and not early:
-                once(m, peak_of)
-            if u == 1 and early:
-                once(m + 1, quantise_h)
-            if u == 2 and early:
-                once(m, pop_less_peak)
-                once(m, pop_less_both)
-                once(m + 1, new_planes)
-                once(m + 1, logit, 2)
-                once(m + 1, logit, 0)
-                once(m + 1, copy_noop)
-            if u == 3 and not early:
-                once(m, store_out)
-                once(m + 1, gap_of)
-                once(m + 1, share_of_push)
-                once(m + 1, larger_share)
-
-        TAIL = LAST - 5
+            if f % TILES == TILES - 1:
+                once(f // TILES, store_out)
 
         def planes_due(k):
             if k < TAIL:
@@ -430,26 +411,72 @@ def tile_stackrnn_pb_t_kernel(
             tile_stage(k, blend_c)
             tile_stage(k, blend_b)
 
-        def slot(k, steps):
+        def chain_first(c):
+            x, phase = c // TILES + 1, c % TILES
+            if phase == 0:
+                once(x + 3, load_h)
+                once(x - 1, share_of_both)
+            if phase == 3:
+                once(x + 2, new_quantise_input)
+
+        def chain_issue(c):
+            x, phase = c // TILES + 1, c % TILES
+            once(x + 1 + (phase + 1) // TILES, transpose_h_tile, (phase + 1) % TILES)
+            if phase == 3 and live(x):
+                load_sigmoid_table()
+            if phase == 1:
+                once(x, logit, 3)
+                once(x, top_of)
+
+        def chain_early(c):
+            x, phase = c // TILES + 1, c % TILES
+            if phase == 0:
+                once(x, quantise_h)
+                once(x, new_planes)
+                once(x, logit, 2)
+                once(x, copy_noop)
+            if phase == 2:
+                once(x, peak_of)
+                once(x, logit, 1)
+                once(x, turn_shares)
+            if phase == 3:
+                once(x, pop_less_peak)
+                once(x, pop_less_both)
+
+        def chain_late(c):
+            x, phase = c // TILES + 1, c % TILES
+            if phase == 1:
+                once(x, gap_of)
+                once(x, share_of_push)
+                once(x, larger_share)
+                once(x, log_of_larger_share)
+
+        def slot(k, chain):
+            phase = chain[0] % TILES
             if k % TILES == 0:
                 once(k // TILES + 2, load_stack)
-            front_issue(steps[0])
+            chain_first(chain[0])
             for ahead in planes_due(k):
                 tile_stage(ahead, turn_planes)
+            chain_issue(chain[0])
             tile_stage(k, blend_e)
-            front_fill(steps[0], True)
-            front_out(steps[0])
+            chain_early(chain[0])
+            front_out(k + OUT_AHEAD)
+            if phase == 0:
+                once(chain[0] // TILES + 1, logit, 0)
             tile_stage(k, blend_d)
+            own = DEPTH
+            stage(k // TILES, blend_f_low, k % TILES, own)
             tile_stage(k + 2, steps_of_stack)
-            front_fill(steps[0], False)
+            chain_late(chain[0])
+            for c in chain[1:]:
+                chain_first(c)
+                chain_issue(c)
+                chain_early(c)
+                chain_late(c)
             begin_tile(k + 1)
-            tile_stage(k, blend_f)
+            stage(k // TILES, blend_f, k % TILES, own)
             tile_stage(k, blend_g)
-            for f in steps[1:]:
-                front_issue(f)
-                front_fill(f, True)
-                front_out(f)
-                front_fill(f, False)
 
         by_vector = nc.vector.tensor_copy
 
@@ -499,25 +526,25 @@ def tile_stackrnn_pb_t_kernel(
         once(0, top_of)
         keep_shares(0, by_vector)
         front_out(1)
+        once(2, new_quantise_input)
+        ahead_of_turn(transpose_h_tile, 2, 0, bank="long", copier=None)
+        ahead_of_turn(transpose_h_tile, 2, 1, bank="planes", copier=None)
         keep_h_tile(1, 2, by_vector)
         keep_h_tile(1, 3, by_vector)
         once(0, share_of_both)
+        for t in range(2):
+            keep_h_tile(2, t, nc.scalar.copy)
         once(1, quantise_h)
-        turn_planes(0, 0)
         steps_of_stack(0, 0)
         steps_of_stack(0, 1)
-        front_out(2)
+        turn_planes(0, 0)
         once(1, new_planes)
         once(1, logit, 2)
-        once(1, logit, 0)
         once(1, copy_noop)
-        once(2, new_quantise_input)
-        once(2, transpose_h_tile, 0)
+        front_out(2)
+        once(1, logit, 0)
+        once(4, load_h)
         begin_tile(0)
-        once(2, transpose_h_tile, 1)
-        slot(0, (3,))
-        slot(1, (4, 5))
-        slot(2, (6,))
-        slot(3, (7, 8))
-        for k in range(4, GROUPS * TILES):
-            slot(k, (k + 5,))
+        slot(0, (1, 2))
+        for k in range(1, GROUPS * TILES):
+            slot(k, (k + CHAIN_AHEAD,))

@@ -67,18 +67,21 @@ def tile_stackrnn_pb_t_kernel(
 
         load_h(0)
 
-        ident = const.tile([P, P], F32)
-        make_identity(nc, ident[:])
-        plus = const.tile([P, P], BF16)
-        nc.vector.tensor_copy(out=plus[:], in_=ident[:])
-        minus = const.tile([P, P], BF16)
-        nc.vector.tensor_scalar_mul(out=minus[:], in0=ident[:], scalar1=-1.0)
-        for st in stack_tiles:
-            nc.vector.memset(st[:, :, DEPTH, :], -1.0)
-
         w_words = const.tile([P, PASSES, W_COLS], U32, align_bytes=64)
         w_planes = const.tile([P, PASSES, W_COLS], U8, align_bytes=64)
         nc.vector.memset(w_planes[:].bitcast(I32), 0)
+        bo_alone = const.tile([P, ODIM], BF16)
+        nc.vector.memset(bo_alone[:], 0.0)
+        bias_rows = const.tile([P, P], BF16)
+        nc.vector.memset(bias_rows[:], 0.0)
+        ones = const.tile([P, P], BF16)
+        nc.vector.memset(ones[:], 1.0)
+        scrap = const.tile([P, 1], F32)
+
+        def load_sigmoid_table():
+            nc.scalar.activation(out=scrap[:], in_=ones[:, 0:1], func=ACT.Sigmoid)
+
+        load_sigmoid_table()
         given = ((Wa_words, Wa_scales, WA_COL, ACTIONS * S), (Ws_words, Ws_scales, WS_COL, S), (Wo_words, Wo_scales, WO_COL, ODIM))
         for words, scales, col, width in given:
             for quad in range(4):
@@ -91,20 +94,21 @@ def tile_stackrnn_pb_t_kernel(
                 out=w_words[:, :, col : col + width].bitcast(I32),
                 in_=words.rearrange("c p n t -> p c (n t)").bitcast(I32),
             )
-
-        bo_alone = const.tile([P, ODIM], BF16)
-        nc.vector.memset(bo_alone[:], 0.0)
         nc.scalar.dma_start(out=bo_alone[0:1, :], in_=bo.rearrange("(a n) -> a n", a=1))
-        ones = const.tile([P, P], BF16)
-        nc.vector.memset(ones[:], 1.0)
-        bo_rows = const.tile([P, ODIM], F32)
-
-        bias_rows = const.tile([P, P], BF16)
-        nc.vector.memset(bias_rows[:], 0.0)
         nc.scalar.dma_start(out=bias_rows[0:ACTIONS, :], in_=ba.rearrange("(a s) -> a s", a=ACTIONS))
         nc.scalar.dma_start(out=bias_rows[ACTIONS : ACTIONS + 1, :], in_=bs.rearrange("(a s) -> a s", a=1))
+        bo_rows = const.tile([P, ODIM], F32)
         bias_rows_f32 = const.tile([P, P], F32)
         bias_col = const.tile([P, ACTIONS + 1], F32)
+
+        ident = const.tile([P, P], F32)
+        make_identity(nc, ident[:])
+        for st in stack_tiles:
+            nc.vector.memset(st[:, :, DEPTH, :], -1.0)
+        plus = const.tile([P, P], BF16)
+        nc.vector.tensor_copy(out=plus[:], in_=ident[:])
+        minus = const.tile([P, P], BF16)
+        nc.vector.tensor_scalar_mul(out=minus[:], in0=ident[:], scalar1=-1.0)
 
         def widen_biases():
             nc.vector.tensor_copy(out=bias_rows_f32[:], in_=bias_rows[:])
@@ -166,11 +170,6 @@ def tile_stackrnn_pb_t_kernel(
                     scales=kept["h_planes", g][:, c, rows],
                     in_=kept["grouped", g][:, c, t, :, :].rearrange("p r j -> p (r j)"),
                 )
-
-        scrap = const.tile([P, 1], F32)
-
-        def load_sigmoid_table():
-            nc.scalar.activation(out=scrap[:], in_=ident[:, 0:1], func=ACT.Sigmoid)
 
         def new_out_tile(g):
             out_sb = work.tile([P, TILES, ODIM], F32)
@@ -340,10 +339,14 @@ def tile_stackrnn_pb_t_kernel(
                 out=kept["inner", g, t][:, 0 : DEPTH - 1, :], in0=kept["steps", g, t][:], in1=kept["scaled", g, t][:, 0 : DEPTH - 1, :], op=ALU.add
             )
 
+        def raise_last_row(g):
+            raised = work.tile([P, TILES, S], F32, bufs=3)
+            nc.gpsimd.tensor_scalar(out=raised[:], in0=kept["st", g][:, :, DEPTH - 1, :], scalar1=1.0, scalar2=1.0, op0=ALU.mult, op1=ALU.add)
+            kept["raised", g] = raised
+
         def blend_e(g, t):
-            nc.vector.scalar_tensor_tensor(
-                out=kept["inner", g, t][:, DEPTH - 1, :], in0=kept["st", g][:, t, DEPTH - 1, :], scalar=1.0,
-                in1=kept["scaled", g, t][:, DEPTH - 1, :], op0=ALU.add, op1=ALU.add,
+            nc.gpsimd.tensor_tensor(
+                out=kept["inner", g, t][:, DEPTH - 1, :], in0=kept["scaled", g, t][:, DEPTH - 1, :], in1=kept["raised", g][:, t, :], op=ALU.add
             )
 
         def blend_f_low(g, t, own):
@@ -363,7 +366,8 @@ def tile_stackrnn_pb_t_kernel(
 
         def blend_g(g, t):
             new = kept["new_sb", g][:, t, :, :]
-            nc.gpsimd.tensor_tensor(out=new, in0=kept["moved", g, t][:], in1=kept["st", g][:, t, 1 : DEPTH + 1, :], op=ALU.add)
+            adder = nc.vector if TILES * g + t == GROUPS * TILES - 1 else nc.gpsimd
+            adder.tensor_tensor(out=new, in0=kept["moved", g, t][:], in1=kept["st", g][:, t, 1 : DEPTH + 1, :], op=ALU.add)
             nc.sync.dma_start(out=out_1[group_rows(g)].rearrange("(p t) d s -> p t d s", t=TILES)[:, t, :, :], in_=new)
 
         def live(g):
@@ -409,6 +413,7 @@ def tile_stackrnn_pb_t_kernel(
         def begin_tile(k):
             tile_stage(k, blend_a)
             tile_stage(k, blend_c)
+            tile_stage(k, blend_e)
             tile_stage(k, blend_b)
 
         def chain_first(c):
@@ -459,7 +464,8 @@ def tile_stackrnn_pb_t_kernel(
             for ahead in planes_due(k):
                 tile_stage(ahead, turn_planes)
             chain_issue(chain[0])
-            tile_stage(k, blend_e)
+            if k % TILES == 0:
+                once(k // TILES + 1, raise_last_row)
             chain_early(chain[0])
             front_out(k + OUT_AHEAD)
             if phase == 0:
@@ -484,7 +490,6 @@ def tile_stackrnn_pb_t_kernel(
             done.add((step, g, args))
             step(g, *args, **how)
 
-        load_sigmoid_table()
         once(1, load_h)
         once(0, new_quantise_input)
         quantise_h_by_tiles(0)
@@ -544,6 +549,7 @@ def tile_stackrnn_pb_t_kernel(
         front_out(2)
         once(1, logit, 0)
         once(4, load_h)
+        once(0, raise_last_row)
         begin_tile(0)
         slot(0, (1, 2))
         for k in range(1, GROUPS * TILES):

@@ -275,68 +275,62 @@ def tile_stackrnn_pb_t_kernel(
         def share_of_both(g):
             nc.scalar.activation(out=kept["planes", g][:, 1, :], in_=kept["odds", g][:], func=ACT.Sigmoid, scale=-1.0)
 
-        def new_stack_tile(g):
-            new_sb = work.tile([P, TILES, DEPTH, S], F32)
-            kept["new_sb", g] = new_sb
-
-        def turn_planes(g, t):
-            if t == 0:
-                new_stack_tile(g)
-            lent = TILES * g + t in (GROUPS * TILES - 4, GROUPS * TILES - 3)
-            planes_t = psum.tile([P, 3, P], F32, tag="quick" if lent else "planes", bufs=2)
-            for j in range(3):
-                nc.tensor.transpose(planes_t[:, j, :], kept["planes", g][:, j, t * P : (t + 1) * P], ident[:])
-            kept["planes_t", g, t] = planes_t
+        def turn_plane(g, j, bank):
+            turned = psum.tile([P, TILES, P], F32, tag=bank, bufs=2)
+            for t in range(TILES):
+                nc.tensor.transpose(turned[:, t, :], kept["planes", g][:, j, t * P : (t + 1) * P], ident[:])
+            kept["turned", g, j] = turned
 
         def turn_shares(g, copier=nc.scalar.copy):
-            shares_t = psum.tile([P, TILES, P], F32, tag="quick", bufs=2)
-            for t in range(TILES):
-                nc.tensor.transpose(shares_t[:, t, :], kept["planes", g][:, 0, t * P : (t + 1) * P], ident[:])
-            kept["shares_t", g] = shares_t
+            turn_plane(g, 0, "pair")
             if copier is not None:
                 keep_shares(g, copier)
 
-        def turn_sums(g):
-            sums_t = psum.tile([P, TILES, P], F32, tag="quick", bufs=2)
-            for t in range(TILES):
-                nc.tensor.transpose(sums_t[:, t, :], kept["planes", g][:, 1, t * P : (t + 1) * P], ident[:])
-            q_sb = work.tile([P, TILES, S], F32, bufs=3)
-            nc.scalar.copy(out=q_sb[:], in_=sums_t[:])
-            kept["q_sb", g] = q_sb
-
         def keep_shares(g, copier):
             p_sb = work.tile([P, TILES, S], F32, bufs=3)
-            copier(out=p_sb[:], in_=kept["shares_t", g][:])
+            copier(out=p_sb[:], in_=kept["turned", g, 0][:])
             kept["p_sb", g] = p_sb
 
-        def steps_of_stack(g, t):
-            st = kept["st", g]
-            steps = psum.tile([P, DEPTH - 1, S], F32, tag="steps", bufs=2)
-            nc.tensor.matmul(out=steps[:], lhsT=plus[:], rhs=st[:, t, 0 : DEPTH - 1, :], start=True, stop=False)
-            nc.tensor.matmul(out=steps[:], lhsT=minus[:], rhs=st[:, t, 1:DEPTH, :], start=False, stop=True)
-            kept["steps", g, t] = steps
+        def turn_tops(g):
+            turn_plane(g, 2, "pair")
 
-        def blend_a(g, t):
-            first = small.tile([P, S], F32)
-            nc.vector.tensor_tensor(out=first[:], in0=kept["planes_t", g, t][:, 2, :], in1=kept["st", g][:, t, 0, :], op=ALU.subtract)
-            kept["first", g, t] = first
-            scaled = small.tile([P, DEPTH, S], F32)
-            kept["scaled", g, t] = scaled
-            inner = small.tile([P, DEPTH, S], F32)
-            kept["inner", g, t] = inner
+        def feed_blend(k):
+            feed = psum.tile([P, DEPTH, S], F32, tag="steps", bufs=2)
+            g, t = (k + 2) // TILES, (k + 2) % TILES
+            if live(g):
+                st = kept["st", g]
+                nc.tensor.matmul(out=feed[:, 0 : DEPTH - 1, :], lhsT=plus[:], rhs=st[:, t, 0 : DEPTH - 1, :], start=True, stop=False)
+                nc.tensor.matmul(out=feed[:, 0 : DEPTH - 1, :], lhsT=minus[:], rhs=st[:, t, 1:DEPTH, :], start=False, stop=True)
+                kept["steps", g, t] = feed
+            g, t = (k + 1) // TILES, (k + 1) % TILES
+            if live(g):
+                nc.tensor.transpose(feed[:, DEPTH - 1, :], kept["planes", g][:, 1, t * P : (t + 1) * P], ident[:])
+                kept["q_t", g, t] = feed
+                if t == 0:
+                    new_sb = work.tile([P, TILES, DEPTH, S], F32)
+                    kept["new_sb", g] = new_sb
 
-        def blend_b(g, t):
-            nc.vector.tensor_tensor(out=kept["scaled", g, t][:, 0, :], in0=kept["planes_t", g, t][:, 0, :], in1=kept["first", g, t][:], op=ALU.mult)
+        def first_steps(g):
+            first = work.tile([P, TILES, S], F32)
+            nc.vector.tensor_tensor(out=first[:], in0=kept["turned", g, 2][:], in1=kept["st", g][:, :, 0, :], op=ALU.subtract)
+            kept["first", g] = first
+
+        def scale_first_steps(g):
+            scaled = work.tile([P, TILES, DEPTH, S], F32, bufs=3)
+            nc.gpsimd.tensor_tensor(out=scaled[:, :, 0, :], in0=kept["p_sb", g][:], in1=kept["first", g][:], op=ALU.mult)
+            kept["scaled", g] = scaled
 
         def blend_c(g, t):
             nc.vector.tensor_tensor(
-                out=kept["scaled", g, t][:, 1:DEPTH, :], in0=kept["steps", g, t][:],
+                out=kept["scaled", g][:, t, 1:DEPTH, :], in0=kept["steps", g, t][:, 0 : DEPTH - 1, :],
                 in1=kept["p_sb", g][:, t, :].unsqueeze(1).to_broadcast([P, DEPTH - 1, S]), op=ALU.mult,
             )
+            inner = small.tile([P, DEPTH, S], F32)
+            kept["inner", g, t] = inner
 
         def blend_d(g, t):
             nc.vector.tensor_tensor(
-                out=kept["inner", g, t][:, 0 : DEPTH - 1, :], in0=kept["steps", g, t][:], in1=kept["scaled", g, t][:, 0 : DEPTH - 1, :], op=ALU.add
+                out=kept["inner", g, t][:, 0 : DEPTH - 1, :], in0=kept["steps", g, t][:, 0 : DEPTH - 1, :], in1=kept["scaled", g][:, t, 0 : DEPTH - 1, :], op=ALU.add
             )
 
         def raise_last_row(g):
@@ -346,23 +340,15 @@ def tile_stackrnn_pb_t_kernel(
 
         def blend_e(g, t):
             nc.gpsimd.tensor_tensor(
-                out=kept["inner", g, t][:, DEPTH - 1, :], in0=kept["scaled", g, t][:, DEPTH - 1, :], in1=kept["raised", g][:, t, :], op=ALU.add
+                out=kept["inner", g, t][:, DEPTH - 1, :], in0=kept["scaled", g][:, t, DEPTH - 1, :], in1=kept["raised", g][:, t, :], op=ALU.add
             )
 
-        def blend_f_low(g, t, own):
+        def blend_f(g, t):
             moved = small.tile([P, DEPTH, S], F32)
-            kept["moved", g, t] = moved
-            if own < DEPTH:
-                nc.gpsimd.tensor_tensor(
-                    out=moved[:, own:DEPTH, :], in0=kept["inner", g, t][:, own:DEPTH, :],
-                    in1=kept["q_sb", g][:, t, :].unsqueeze(1).to_broadcast([P, DEPTH - own, S]), op=ALU.mult,
-                )
-
-        def blend_f(g, t, own):
             nc.vector.tensor_tensor(
-                out=kept["moved", g, t][:, 0:own, :], in0=kept["planes_t", g, t][:, 1, :].unsqueeze(1).to_broadcast([P, own, S]),
-                in1=kept["inner", g, t][:, 0:own, :], op=ALU.mult,
+                out=moved[:], in0=kept["q_t", g, t][:, DEPTH - 1, :].unsqueeze(1).to_broadcast([P, DEPTH, S]), in1=kept["inner", g, t][:], op=ALU.mult
             )
+            kept["moved", g, t] = moved
 
         def blend_g(g, t):
             new = kept["new_sb", g][:, t, :, :]
@@ -378,10 +364,8 @@ def tile_stackrnn_pb_t_kernel(
                 step(g, *args)
 
         done = set()
-        LAST = GROUPS * TILES - 1
         OUT_AHEAD = 3
         CHAIN_AHEAD = 2
-        TAIL = LAST - 3 - CHAIN_AHEAD
 
         def once(g, step, *args):
             if live(g) and (step, g, args) not in done:
@@ -403,24 +387,17 @@ def tile_stackrnn_pb_t_kernel(
             if f % TILES == TILES - 1:
                 once(f // TILES, store_out)
 
-        def planes_due(k):
-            if k < TAIL:
-                return (k + 1,)
-            if k == TAIL:
-                return (k + 1, k + 2)
-            return (k + 2,)
-
         def begin_tile(k):
-            tile_stage(k, blend_a)
             tile_stage(k, blend_c)
             tile_stage(k, blend_e)
-            tile_stage(k, blend_b)
 
         def chain_first(c):
             x, phase = c // TILES + 1, c % TILES
             if phase == 0:
                 once(x + 3, load_h)
                 once(x - 1, share_of_both)
+            if phase == 2:
+                once(x, turn_tops)
             if phase == 3:
                 once(x + 2, new_quantise_input)
 
@@ -455,25 +432,27 @@ def tile_stackrnn_pb_t_kernel(
                 once(x, share_of_push)
                 once(x, larger_share)
                 once(x, log_of_larger_share)
+            if phase == 3:
+                once(x, scale_first_steps)
 
         def slot(k, chain):
             phase = chain[0] % TILES
             if k % TILES == 0:
                 once(k // TILES + 2, load_stack)
             chain_first(chain[0])
-            for ahead in planes_due(k):
-                tile_stage(ahead, turn_planes)
             chain_issue(chain[0])
             if k % TILES == 0:
                 once(k // TILES + 1, raise_last_row)
             chain_early(chain[0])
-            front_out(k + OUT_AHEAD)
+            if phase != 1:
+                front_out(k + OUT_AHEAD)
             if phase == 0:
                 once(chain[0] // TILES + 1, logit, 0)
             tile_stage(k, blend_d)
-            own = DEPTH
-            stage(k // TILES, blend_f_low, k % TILES, own)
-            tile_stage(k + 2, steps_of_stack)
+            if phase == 1:
+                front_out(k + OUT_AHEAD)
+            if k < GROUPS * TILES - 1:
+                feed_blend(k)
             chain_late(chain[0])
             for c in chain[1:]:
                 chain_first(c)
@@ -481,7 +460,10 @@ def tile_stackrnn_pb_t_kernel(
                 chain_early(c)
                 chain_late(c)
             begin_tile(k + 1)
-            stage(k // TILES, blend_f, k % TILES, own)
+            for c in chain:
+                if c % TILES == 2:
+                    once(c // TILES + 1, first_steps)
+            tile_stage(k, blend_f)
             tile_stage(k, blend_g)
 
         by_vector = nc.vector.tensor_copy
@@ -495,7 +477,7 @@ def tile_stackrnn_pb_t_kernel(
         quantise_h_by_tiles(0)
         done.add((quantise_h, 0, ()))
         for t in range(TILES):
-            transpose_h_tile(0, t, "planes" if t % 2 else "quick")
+            transpose_h_tile(0, t, "pair" if t % 2 else "quick")
             quantise_h_tile(0, t)
             if t == 0:
                 widen_biases()
@@ -512,8 +494,8 @@ def tile_stackrnn_pb_t_kernel(
         once(0, copy_noop)
         once(0, logit, 3)
         front_prepare(0)
-        ahead_of_turn(transpose_h_tile, 1, 0, bank="planes", copier=None)
-        ahead_of_turn(transpose_h_tile, 1, 1, bank="planes", copier=None)
+        ahead_of_turn(transpose_h_tile, 1, 0, bank="pair", copier=None)
+        ahead_of_turn(transpose_h_tile, 1, 1, bank="pair", copier=None)
         once(0, gap_of)
         once(0, peak_of)
         once(0, share_of_push)
@@ -533,16 +515,18 @@ def tile_stackrnn_pb_t_kernel(
         front_out(1)
         once(2, new_quantise_input)
         ahead_of_turn(transpose_h_tile, 2, 0, bank="long", copier=None)
-        ahead_of_turn(transpose_h_tile, 2, 1, bank="planes", copier=None)
+        ahead_of_turn(transpose_h_tile, 2, 1, bank="pair", copier=None)
         keep_h_tile(1, 2, by_vector)
         keep_h_tile(1, 3, by_vector)
+        once(0, turn_tops)
         once(0, share_of_both)
         for t in range(2):
             keep_h_tile(2, t, nc.scalar.copy)
         once(1, quantise_h)
-        steps_of_stack(0, 0)
-        steps_of_stack(0, 1)
-        turn_planes(0, 0)
+        feed_blend(-2)
+        feed_blend(-1)
+        once(0, first_steps)
+        once(0, scale_first_steps)
         once(1, new_planes)
         once(1, logit, 2)
         once(1, copy_noop)

@@ -335,7 +335,7 @@ def tile_stackrnn_pb_t_kernel(
 
         def raise_last_row(g):
             raised = work.tile([P, TILES, S], F32, bufs=3)
-            nc.gpsimd.tensor_scalar(out=raised[:], in0=kept["st", g][:, :, DEPTH - 1, :], scalar1=1.0, scalar2=1.0, op0=ALU.mult, op1=ALU.add)
+            nc.scalar.activation(out=raised[:], in_=kept["st", g][:, :, DEPTH - 1, :], func=ACT.Identity, bias=1.0, scale=1.0)
             kept["raised", g] = raised
 
         def blend_e(g, t):
@@ -432,8 +432,8 @@ def tile_stackrnn_pb_t_kernel(
                 once(x, share_of_push)
                 once(x, larger_share)
                 once(x, log_of_larger_share)
-            if phase == 3:
-                once(x, scale_first_steps)
+            if phase == 1:
+                once(x - 1, scale_first_steps)
 
         def slot(k, chain):
             phase = chain[0] % TILES

@@ -353,7 +353,8 @@ def tile_stackrnn_pb_t_kernel(
         def blend_g(g, t):
             new = kept["new_sb", g][:, t, :, :]
             adder = nc.vector if TILES * g + t == GROUPS * TILES - 1 else nc.gpsimd
-            adder.tensor_tensor(out=new, in0=kept["moved", g, t][:], in1=kept["st", g][:, t, 1 : DEPTH + 1, :], op=ALU.add)
+            adder.tensor_tensor(out=new[:, 0 : DEPTH - 1, :], in0=kept["moved", g, t][:, 0 : DEPTH - 1, :], in1=kept["st", g][:, t, 1:DEPTH, :], op=ALU.add)
+            nc.scalar.activation(out=new[:, DEPTH - 1, :], in_=kept["moved", g, t][:, DEPTH - 1, :], func=ACT.Identity, bias=-1.0, scale=1.0)
             nc.sync.dma_start(out=out_1[group_rows(g)].rearrange("(p t) d s -> p t d s", t=TILES)[:, t, :, :], in_=new)
 
         def live(g):

@@ -27,7 +27,6 @@ WA_COL = 0
 WS_COL = WA_COL + ACTIONS * S
 WO_COL = WS_COL + S
 W_COLS = WO_COL + ODIM
-STACK_BUFS = 3
 
 FLOPS = 2 * ROWS * K * W_COLS
 
@@ -56,13 +55,9 @@ def tile_stackrnn_pb_t_kernel(
                 nc.sync.dma_start(out=x[:, t, :], in_=rows[:, t, :])
             kept["x", g] = x
 
-        stack_tiles = [const.tile([P, TILES, DEPTH + 1, S], BF16, name="stack%d" % i) for i in range(STACK_BUFS)]
-
         def load_stack(g):
-            st = stack_tiles[g % STACK_BUFS]
-            nc.sync.dma_start(
-                out=st[:, :, 0:DEPTH, :], in_=stack[group_rows(g)].rearrange("(p t) d s -> p t d s", t=TILES)
-            )
+            st = loads.tile([P, TILES, DEPTH, S], BF16)
+            nc.sync.dma_start(out=st[:], in_=stack[group_rows(g)].rearrange("(p t) d s -> p t d s", t=TILES))
             kept["st", g] = st
 
         load_h(0)
@@ -103,8 +98,6 @@ def tile_stackrnn_pb_t_kernel(
 
         ident = const.tile([P, P], F32)
         make_identity(nc, ident[:])
-        for st in stack_tiles:
-            nc.vector.memset(st[:, :, DEPTH, :], -1.0)
         plus = const.tile([P, P], BF16)
         nc.vector.tensor_copy(out=plus[:], in_=ident[:])
         minus = const.tile([P, P], BF16)
@@ -320,7 +313,7 @@ def tile_stackrnn_pb_t_kernel(
             nc.gpsimd.tensor_tensor(out=scaled[:, :, 0, :], in0=kept["p_sb", g][:], in1=kept["first", g][:], op=ALU.mult)
             kept["scaled", g] = scaled
 
-        def blend_c(g, t):
+        def scale_steps(g, t):
             nc.vector.tensor_tensor(
                 out=kept["scaled", g][:, t, 1:DEPTH, :], in0=kept["steps", g, t][:, 0 : DEPTH - 1, :],
                 in1=kept["p_sb", g][:, t, :].unsqueeze(1).to_broadcast([P, DEPTH - 1, S]), op=ALU.mult,
@@ -328,9 +321,10 @@ def tile_stackrnn_pb_t_kernel(
             inner = small.tile([P, DEPTH, S], F32)
             kept["inner", g, t] = inner
 
-        def blend_d(g, t):
+        def inner_sums(g, t):
             nc.vector.tensor_tensor(
-                out=kept["inner", g, t][:, 0 : DEPTH - 1, :], in0=kept["steps", g, t][:, 0 : DEPTH - 1, :], in1=kept["scaled", g][:, t, 0 : DEPTH - 1, :], op=ALU.add
+                out=kept["inner", g, t][:, 0 : DEPTH - 1, :], in0=kept["steps", g, t][:, 0 : DEPTH - 1, :],
+                in1=kept["scaled", g][:, t, 0 : DEPTH - 1, :], op=ALU.add,
             )
 
         def raise_last_row(g):
@@ -338,23 +332,28 @@ def tile_stackrnn_pb_t_kernel(
             nc.scalar.activation(out=raised[:], in_=kept["st", g][:, :, DEPTH - 1, :], func=ACT.Identity, bias=1.0, scale=1.0)
             kept["raised", g] = raised
 
-        def blend_e(g, t):
+        def last_inner_sum(g, t):
             nc.gpsimd.tensor_tensor(
-                out=kept["inner", g, t][:, DEPTH - 1, :], in0=kept["scaled", g][:, t, DEPTH - 1, :], in1=kept["raised", g][:, t, :], op=ALU.add
+                out=kept["inner", g, t][:, DEPTH - 1, :], in0=kept["scaled", g][:, t, DEPTH - 1, :],
+                in1=kept["raised", g][:, t, :], op=ALU.add,
             )
 
-        def blend_f(g, t):
+        def scale_by_q(g, t):
             moved = small.tile([P, DEPTH, S], F32)
             nc.vector.tensor_tensor(
-                out=moved[:], in0=kept["q_t", g, t][:, DEPTH - 1, :].unsqueeze(1).to_broadcast([P, DEPTH, S]), in1=kept["inner", g, t][:], op=ALU.mult
+                out=moved[:], in0=kept["q_t", g, t][:, DEPTH - 1, :].unsqueeze(1).to_broadcast([P, DEPTH, S]),
+                in1=kept["inner", g, t][:], op=ALU.mult,
             )
             kept["moved", g, t] = moved
 
-        def blend_g(g, t):
+        def add_popped_and_store(g, t):
             new = kept["new_sb", g][:, t, :, :]
             adder = nc.vector if TILES * g + t == GROUPS * TILES - 1 else nc.gpsimd
-            adder.tensor_tensor(out=new[:, 0 : DEPTH - 1, :], in0=kept["moved", g, t][:, 0 : DEPTH - 1, :], in1=kept["st", g][:, t, 1:DEPTH, :], op=ALU.add)
-            nc.scalar.activation(out=new[:, DEPTH - 1, :], in_=kept["moved", g, t][:, DEPTH - 1, :], func=ACT.Identity, bias=-1.0, scale=1.0)
+            moved = kept["moved", g, t]
+            adder.tensor_tensor(
+                out=new[:, 0 : DEPTH - 1, :], in0=moved[:, 0 : DEPTH - 1, :], in1=kept["st", g][:, t, 1:DEPTH, :], op=ALU.add
+            )
+            nc.scalar.activation(out=new[:, DEPTH - 1, :], in_=moved[:, DEPTH - 1, :], func=ACT.Identity, bias=-1.0, scale=1.0)
             nc.sync.dma_start(out=out_1[group_rows(g)].rearrange("(p t) d s -> p t d s", t=TILES)[:, t, :, :], in_=new)
 
         def live(g):
@@ -389,8 +388,8 @@ def tile_stackrnn_pb_t_kernel(
                 once(f // TILES, store_out)
 
         def begin_tile(k):
-            tile_stage(k, blend_c)
-            tile_stage(k, blend_e)
+            tile_stage(k, scale_steps)
+            tile_stage(k, last_inner_sum)
 
         def chain_first(c):
             x, phase = c // TILES + 1, c % TILES
@@ -433,7 +432,6 @@ def tile_stackrnn_pb_t_kernel(
                 once(x, share_of_push)
                 once(x, larger_share)
                 once(x, log_of_larger_share)
-            if phase == 1:
                 once(x - 1, scale_first_steps)
 
         def slot(k, chain):
@@ -449,7 +447,7 @@ def tile_stackrnn_pb_t_kernel(
                 front_out(k + OUT_AHEAD)
             if phase == 0:
                 once(chain[0] // TILES + 1, logit, 0)
-            tile_stage(k, blend_d)
+            tile_stage(k, inner_sums)
             if phase == 1:
                 front_out(k + OUT_AHEAD)
             if k < GROUPS * TILES - 1:
@@ -464,8 +462,8 @@ def tile_stackrnn_pb_t_kernel(
             for c in chain:
                 if c % TILES == 2:
                     once(c // TILES + 1, first_steps)
-            tile_stage(k, blend_f)
-            tile_stage(k, blend_g)
+            tile_stage(k, scale_by_q)
+            tile_stage(k, add_popped_and_store)
 
         by_vector = nc.vector.tensor_copy
 

@@ -77,14 +77,13 @@ def tile_stackrnn_pb_t_kernel(
             nc.scalar.activation(out=scrap[:], in_=ones[:, 0:1], func=ACT.Sigmoid)
 
         load_sigmoid_table()
-        given = ((Wa_words, Wa_scales, WA_COL, ACTIONS * S), (Ws_words, Ws_scales, WS_COL, S), (Wo_words, Wo_scales, WO_COL, ODIM))
+        given = ((Wa_words, Wa_scales, WA_COL, ACTIONS * S), (Wo_words, Wo_scales, WO_COL, ODIM), (Ws_words, Ws_scales, WS_COL, S))
         for words, scales, col, width in given:
             for quad in range(4):
                 nc.sync.dma_start(
                     out=w_planes[32 * quad : 32 * quad + 4, :, col : col + width].bitcast(I32),
                     in_=scales[:, 4 * quad : 4 * quad + 4, :].rearrange("c r n -> r c n").bitcast(I32),
                 )
-        for words, scales, col, width in given:
             nc.sync.dma_start(
                 out=w_words[:, :, col : col + width].bitcast(I32),
                 in_=words.rearrange("c p n t -> p c (n t)").bitcast(I32),
@@ -138,6 +137,11 @@ def tile_stackrnn_pb_t_kernel(
                 in_=kept["h_t", g, t][:].rearrange("p c u r -> p c r u"),
             )
 
+        def keep_h_tile_alone(g, t):
+            alone = const.tile([P, PASSES, P, 4], BF16, align_bytes=64, name="alone%d" % t)
+            nc.scalar.copy(out=alone[:].bitcast(F32), in_=kept["h_t", g, t][:].rearrange("p c u r -> p c r u"))
+            kept["alone", g, t] = alone
+
         def quantise_h(g):
             h_words = work.tile([P, PASSES, GROUP], U32, align_bytes=64)
             h_planes = work.tile([P, PASSES, GROUP], U8, align_bytes=64)
@@ -161,7 +165,7 @@ def tile_stackrnn_pb_t_kernel(
                 nc.vector.quantize_mx(
                     out=kept["h_words", g][:, c, rows].bitcast(FP8X4),
                     scales=kept["h_planes", g][:, c, rows],
-                    in_=kept["grouped", g][:, c, t, :, :].rearrange("p r j -> p (r j)"),
+                    in_=kept["alone", g, t][:, c, :, :].rearrange("p r j -> p (r j)"),
                 )
 
         def new_out_tile(g):
@@ -472,11 +476,11 @@ def tile_stackrnn_pb_t_kernel(
             step(g, *args, **how)
 
         once(1, load_h)
-        once(0, new_quantise_input)
         quantise_h_by_tiles(0)
         done.add((quantise_h, 0, ()))
         for t in range(TILES):
-            transpose_h_tile(0, t, "pair" if t % 2 else "quick")
+            transpose_h_tile(0, t, "pair" if t % 2 else "quick", copier=None)
+            keep_h_tile_alone(0, t)
             quantise_h_tile(0, t)
             if t == 0:
                 widen_biases()
@@ -491,7 +495,6 @@ def tile_stackrnn_pb_t_kernel(
         once(0, logit, 2)
         once(0, logit, 0)
         once(0, copy_noop)
-        once(0, logit, 3)
         front_prepare(0)
         ahead_of_turn(transpose_h_tile, 1, 0, bank="pair", copier=None)
         ahead_of_turn(transpose_h_tile, 1, 1, bank="pair", copier=None)
@@ -500,6 +503,7 @@ def tile_stackrnn_pb_t_kernel(
         once(0, share_of_push)
         once(0, larger_share)
         once(0, logit, 1)
+        once(0, logit, 3)
         ahead_of_turn(turn_shares, 0, copier=None)
         front_out(0)
         keep_h_tile(1, 0, by_vector)

from contextlib import ExitStack

import concourse.mybir as mybir
from concourse.masks import make_identity

F32 = mybir.dt.float32
BF16 = mybir.dt.bfloat16
I32 = mybir.dt.int32
U32 = mybir.dt.uint32
U8 = mybir.dt.uint8
FP8X4 = mybir.dt.float8_e4m3fn_x4
ALU = mybir.AluOpType
ACT = mybir.ActivationFunctionType

P = 128
ROWS = 4096
K = 1024
PASSES = K // (4 * P)
S = 128
DEPTH = 4
ACTIONS = 3
ODIM = 512
TILES = 4
GROUP = TILES * P
GROUPS = ROWS // GROUP
WA_COL = 0
WS_COL = WA_COL + ACTIONS * S
WO_COL = WS_COL + S
W_COLS = WO_COL + ODIM

FLOPS = 2 * ROWS * K * W_COLS


def tile_stackrnn_pb_t_kernel(
    tc, h, stack, Wa_words, Wa_scales, ba, Ws_words, Ws_scales, bs, Wo_words, Wo_scales, bo, out_0, out_1
):
    nc = tc.nc
    with ExitStack() as pools:
        const = pools.enter_context(tc.tile_pool(name="const", bufs=1))
        loads = pools.enter_context(tc.tile_pool(name="loads", bufs=3))
        work = pools.enter_context(tc.tile_pool(name="work", bufs=2))
        small = pools.enter_context(tc.tile_pool(name="small", bufs=3))
        psum = pools.enter_context(tc.psum_pool(name="psum", bufs=1))
        pools.enter_context(tc.manual_schedule())

        def group_rows(g):
            return slice(g * GROUP, (g + 1) * GROUP)

        kept = {}

        def load_h(g):
            x = loads.tile([P, TILES, K], BF16)
            rows = h[group_rows(g), :].rearrange("(p t) k -> p t k", t=TILES)
            for t in range(TILES):
                nc.sync.dma_start(out=x[:, t, :], in_=rows[:, t, :])
            kept["x", g] = x

        def load_stack(g):
            st = loads.tile([P, TILES, DEPTH, S], BF16)
            nc.sync.dma_start(out=st[:], in_=stack[group_rows(g)].rearrange("(p t) d s -> p t d s", t=TILES))
            kept["st", g] = st

        load_h(0)

        w_words = const.tile([P, PASSES, W_COLS], U32, align_bytes=64)
        w_planes = const.tile([P, PASSES, W_COLS], U8, align_bytes=64)
        nc.vector.memset(w_planes[:].bitcast(I32), 0)
        bo_alone = const.tile([P, ODIM], BF16)
        nc.vector.memset(bo_alone[:], 0.0)
        bias_rows = const.tile([P, P], BF16)
        nc.vector.memset(bias_rows[:], 0.0)
        ones = const.tile([P, P], BF16)
        nc.vector.memset(ones[:], 1.0)
        scrap = const.tile([P, 1], F32)

        def load_sigmoid_table():
            nc.scalar.activation(out=scrap[:], in_=ones[:, 0:1], func=ACT.Sigmoid)

        load_sigmoid_table()
        given = ((Wa_words, Wa_scales, WA_COL, ACTIONS * S), (Wo_words, Wo_scales, WO_COL, ODIM), (Ws_words, Ws_scales, WS_COL, S))
        for words, scales, col, width in given:
            for quad in range(4):
                nc.sync.dma_start(
                    out=w_planes[32 * quad : 32 * quad + 4, :, col : col + width].bitcast(I32),
                    in_=scales[:, 4 * quad : 4 * quad + 4, :].rearrange("c r n -> r c n").bitcast(I32),
                )
            nc.sync.dma_start(
                out=w_words[:, :, col : col + width].bitcast(I32),
                in_=words.rearrange("c p n t -> p c (n t)").bitcast(I32),
            )
        nc.scalar.dma_start(out=bo_alone[0:1, :], in_=bo.rearrange("(a n) -> a n", a=1))
        nc.scalar.dma_start(out=bias_rows[0:ACTIONS, :], in_=ba.rearrange("(a s) -> a s", a=ACTIONS))
        nc.scalar.dma_start(out=bias_rows[ACTIONS : ACTIONS + 1, :], in_=bs.rearrange("(a s) -> a s", a=1))
        bo_rows = const.tile([P, ODIM], F32)
        bias_rows_f32 = const.tile([P, P], F32)
        bias_col = const.tile([P, ACTIONS + 1], F32)

        ident = const.tile([P, P], F32)
        make_identity(nc, ident[:])
        plus = const.tile([P, P], BF16)
        nc.vector.tensor_copy(out=plus[:], in_=ident[:])
        minus = const.tile([P, P], BF16)
        nc.vector.tensor_scalar_mul(out=minus[:], in0=ident[:], scalar1=-1.0)

        def widen_biases():
            nc.vector.tensor_copy(out=bias_rows_f32[:], in_=bias_rows[:])

        def turn_biases():
            bias_t = psum.tile([P, ACTIONS + 1, P], F32, tag="steps", bufs=2)
            nc.tensor.transpose(bias_t[:, 0, :], bias_rows_f32[:], ident[:])
            bo_spread = psum.tile([P, ODIM], F32, tag="steps", bufs=2)
            nc.tensor.matmul(out=bo_spread[:], lhsT=ones[:], rhs=bo_alone[:], start=True, stop=True)
            kept["bias_t"] = bias_t
            kept["bo_spread"] = bo_spread

        def keep_biases():
            nc.vector.tensor_copy(out=bias_col[:], in_=kept["bias_t"][:, 0, 0 : ACTIONS + 1])
            nc.vector.tensor_copy(out=bo_rows[:], in_=kept["bo_spread"][:])

        def new_quantise_input(g):
            grouped = work.tile([P, PASSES, TILES, P, 4], BF16, align_bytes=64)
            kept["grouped", g] = grouped

        def transpose_h_tile(g, t, bank="quick", copier=nc.scalar.copy):
            words = kept["x", g][:, t, :].bitcast(F32)
            h_t = psum.tile([P, PASSES, 2, P], F32, tag=bank, bufs=1 if bank == "long" else 2)
            for c in range(PASSES):
                for u in range(2):
                    nc.tensor.transpose(h_t[:, c, u, :], words[:, 256 * c + u : 256 * (c + 1) : 2], ident[:])
            kept["h_t", g, t] = h_t
            if copier is not None:
                keep_h_tile(g, t, copier)

        def keep_h_tile(g, t, copier):
            copier(
                out=kept["grouped", g][:].bitcast(F32)[:, :, t, :, :],
                in_=kept["h_t", g, t][:].rearrange("p c u r -> p c r u"),
            )

        def keep_h_tile_alone(g, t):
            alone = const.tile([P, PASSES, P, 4], BF16, align_bytes=64, name="alone%d" % t)
            nc.scalar.copy(out=alone[:].bitcast(F32), in_=kept["h_t", g, t][:].rearrange("p c u r -> p c r u"))
            kept["alone", g, t] = alone

        def quantise_h(g):
            h_words = work.tile([P, PASSES, GROUP], U32, align_bytes=64)
            h_planes = work.tile([P, PASSES, GROUP], U8, align_bytes=64)
            nc.vector.quantize_mx(
                out=h_words[:].rearrange("p c r -> p (c r)").bitcast(FP8X4),
                scales=h_planes[:].rearrange("p c r -> p (c r)"),
                in_=kept["grouped", g][:].rearrange("p c t r j -> p (c t r j)"),
            )
            kept["h_words", g] = h_words
            kept["h_planes", g] = h_planes

        def quantise_h_by_tiles(g):
            h_words = work.tile([P, PASSES, GROUP], U32, align_bytes=64)
            h_planes = work.tile([P, PASSES, GROUP], U8, align_bytes=64)
            kept["h_words", g] = h_words
            kept["h_planes", g] = h_planes

        def quantise_h_tile(g, t):
            rows = slice(t * P, (t + 1) * P)
            for c in range(PASSES):
                nc.vector.quantize_mx(
                    out=kept["h_words", g][:, c, rows].bitcast(FP8X4),
                    scales=kept["h_planes", g][:, c, rows],
                    in_=kept["alone", g, t][:, c, :, :].rearrange("p r j -> p (r j)"),
                )

        def new_out_tile(g):
            out_sb = work.tile([P, TILES, ODIM], F32)
            kept["out_sb", g] = out_sb

        def out_passes(g, t):
            rows = slice(t * P, (t + 1) * P)
            acc = psum.tile([P, ODIM], F32, tag="out", bufs=1)
            for c in range(PASSES):
                nc.tensor.matmul_mx(
                    out=acc[:],
                    lhsT=kept["h_words", g][:, c, rows].bitcast(FP8X4),
                    lhsT_scale=kept["h_planes", g][:, c, rows],
                    rhs=w_words[:, c, WO_COL:W_COLS].bitcast(FP8X4),
                    rhs_scale=w_planes[:, c, WO_COL:W_COLS],
                    start=(c == 0),
                    stop=(c == PASSES - 1),
                )
            kept["out_acc", g, t] = acc

        def out_bias(g, t):
            nc.vector.tensor_tensor(
                out=kept["out_sb", g][:, t, :], in0=kept["out_acc", g, t][:], in1=bo_rows[:], op=ALU.add
            )

        def store_out(g):
            nc.sync.dma_start(
                out=out_0[group_rows(g), :].rearrange("(p t) n -> p t n", t=TILES), in_=kept["out_sb", g][:]
            )

        def logit(g, j):
            long_lived = j in (0, 1)
            acc = psum.tile([P, GROUP], F32, tag="long" if long_lived else "quick", bufs=1 if long_lived else 2)
            cols = slice(j * S, (j + 1) * S)
            for c in range(PASSES):
                nc.tensor.matmul_mx(
                    out=acc[:],
                    lhsT=w_words[:, c, cols].bitcast(FP8X4),
                    lhsT_scale=w_planes[:, c, cols],
                    rhs=kept["h_words", g][:, c, :].bitcast(FP8X4),
                    rhs_scale=kept["h_planes", g][:, c, :],
                    start=(c == 0),
                    stop=(c == PASSES - 1),
                )
            kept["logit%d" % j, g] = acc

        def new_planes(g):
            planes = work.tile([P, 3, GROUP], F32, bufs=3)
            kept["planes", g] = planes

        def copy_noop(g):
            noop = work.tile([P, GROUP], F32)
            nc.scalar.activation(out=noop[:], in_=kept["logit2", g][:], func=ACT.Identity, bias=bias_col[:, 2:3], scale=1.0)
            kept["noop", g] = noop

        def top_of(g):
            nc.scalar.activation(
                out=kept["planes", g][:, 2, :], in_=kept["logit3", g][:], func=ACT.Sigmoid, bias=bias_col[:, 3:4], scale=1.0
            )

        def gap_of(g):
            gap = work.tile([P, GROUP], F32)
            nc.vector.scalar_tensor_tensor(
                out=gap[:], in0=kept["logit0", g][:], scalar=bias_col[:, 0:1], in1=kept["noop", g][:],
                op0=ALU.add, op1=ALU.subtract,
            )
            kept["gap", g] = gap

        def peak_of(g):
            peak = work.tile([P, GROUP], F32)
            nc.vector.scalar_tensor_tensor(
                out=peak[:], in0=kept["logit0", g][:], scalar=bias_col[:, 0:1], in1=kept["noop", g][:],
                op0=ALU.add, op1=ALU.max,
            )
            kept["peak", g] = peak

        def pop_less_peak(g):
            below = work.tile([P, GROUP], F32)
            nc.vector.scalar_tensor_tensor(
                out=below[:], in0=kept["logit1", g][:], scalar=bias_col[:, 1:2], in1=kept["peak", g][:],
                op0=ALU.add, op1=ALU.subtract,
            )
            kept["below", g] = below

        def share_of_push(g):
            nc.scalar.activation(out=kept["planes", g][:, 0, :], in_=kept["gap", g][:], func=ACT.Sigmoid)

        def larger_share(g):
            off_half = work.tile([P, GROUP], F32)
            nc.scalar.activation(out=off_half[:], in_=kept["planes", g][:, 0, :], func=ACT.Abs, bias=-0.5, scale=1.0)
            kept["off_half", g] = off_half

        def log_of_larger_share(g):
            log_share = work.tile([P, GROUP], F32)
            nc.scalar.activation(out=log_share[:], in_=kept["off_half", g][:], func=ACT.Ln, bias=0.5, scale=1.0)
            kept["log_share", g] = log_share

        def pop_less_both(g):
            odds = work.tile([P, GROUP], F32)
            nc.gpsimd.tensor_tensor(out=odds[:], in0=kept["below", g][:], in1=kept["log_share", g][:], op=ALU.add)
            kept["odds", g] = odds

        def share_of_both(g):
            nc.scalar.activation(out=kept["planes", g][:, 1, :], in_=kept["odds", g][:], func=ACT.Sigmoid, scale=-1.0)

        def turn_plane(g, j, bank):
            turned = psum.tile([P, TILES, P], F32, tag=bank, bufs=2)
            for t in range(TILES):
                nc.tensor.transpose(turned[:, t, :], kept["planes", g][:, j, t * P : (t + 1) * P], ident[:])
            kept["turned", g, j] = turned

        def turn_shares(g, copier=nc.scalar.copy):
            turn_plane(g, 0, "pair")
            if copier is not None:
                keep_shares(g, copier)

        def keep_shares(g, copier):
            p_sb = work.tile([P, TILES, S], F32, bufs=3)
            copier(out=p_sb[:], in_=kept["turned", g, 0][:])
            kept["p_sb", g] = p_sb

        def turn_tops(g):
            turn_plane(g, 2, "pair")

        def feed_blend(k):
            feed = psum.tile([P, DEPTH, S], F32, tag="steps", bufs=2)
            g, t = (k + 2) // TILES, (k + 2) % TILES
            if live(g):
                st = kept["st", g]
                nc.tensor.matmul(out=feed[:, 0 : DEPTH - 1, :], lhsT=plus[:], rhs=st[:, t, 0 : DEPTH - 1, :], start=True, stop=False)
                nc.tensor.matmul(out=feed[:, 0 : DEPTH - 1, :], lhsT=minus[:], rhs=st[:, t, 1:DEPTH, :], start=False, stop=True)
                kept["steps", g, t] = feed
            g, t = (k + 1) // TILES, (k + 1) % TILES
            if live(g):
                nc.tensor.transpose(feed[:, DEPTH - 1, :], kept["planes", g][:, 1, t * P : (t + 1) * P], ident[:])
                kept["q_t", g, t] = feed
                if t == 0:
                    new_sb = work.tile([P, TILES, DEPTH, S], F32)
                    kept["new_sb", g] = new_sb

        def first_steps(g):
            first = work.tile([P, TILES, S], F32)
            nc.vector.tensor_tensor(out=first[:], in0=kept["turned", g, 2][:], in1=kept["st", g][:, :, 0, :], op=ALU.subtract)
            kept["first", g] = first

        def scale_first_steps(g):
            scaled = work.tile([P, TILES, DEPTH, S], F32, bufs=3)
            nc.gpsimd.tensor_tensor(out=scaled[:, :, 0, :], in0=kept["p_sb", g][:], in1=kept["first", g][:], op=ALU.mult)
            kept["scaled", g] = scaled

        def scale_steps(g, t):
            nc.vector.tensor_tensor(
                out=kept["scaled", g][:, t, 1:DEPTH, :], in0=kept["steps", g, t][:, 0 : DEPTH - 1, :],
                in1=kept["p_sb", g][:, t, :].unsqueeze(1).to_broadcast([P, DEPTH - 1, S]), op=ALU.mult,
            )
            inner = small.tile([P, DEPTH, S], F32)
            kept["inner", g, t] = inner

        def inner_sums(g, t):
            nc.vector.tensor_tensor(
                out=kept["inner", g, t][:, 0 : DEPTH - 1, :], in0=kept["steps", g, t][:, 0 : DEPTH - 1, :],
                in1=kept["scaled", g][:, t, 0 : DEPTH - 1, :], op=ALU.add,
            )

        def raise_last_row(g):
            raised = work.tile([P, TILES, S], F32, bufs=3)
            nc.scalar.activation(out=raised[:], in_=kept["st", g][:, :, DEPTH - 1, :], func=ACT.Identity, bias=1.0, scale=1.0)
            kept["raised", g] = raised

        def last_inner_sum(g, t):
            nc.gpsimd.tensor_tensor(
                out=kept["inner", g, t][:, DEPTH - 1, :], in0=kept["scaled", g][:, t, DEPTH - 1, :],
                in1=kept["raised", g][:, t, :], op=ALU.add,
            )

        def scale_by_q(g, t):
            moved = small.tile([P, DEPTH, S], F32)
            nc.vector.tensor_tensor(
                out=moved[:], in0=kept["q_t", g, t][:, DEPTH - 1, :].unsqueeze(1).to_broadcast([P, DEPTH, S]),
                in1=kept["inner", g, t][:], op=ALU.mult,
            )
            kept["moved", g, t] = moved

        def add_popped_and_store(g, t):
            new = kept["new_sb", g][:, t, :, :]
            adder = nc.vector if TILES * g + t == GROUPS * TILES - 1 else nc.gpsimd
            moved = kept["moved", g, t]
            adder.tensor_tensor(
                out=new[:, 0 : DEPTH - 1, :], in0=moved[:, 0 : DEPTH - 1, :], in1=kept["st", g][:, t, 1:DEPTH, :], op=ALU.add
            )
            nc.scalar.activation(out=new[:, DEPTH - 1, :], in_=moved[:, DEPTH - 1, :], func=ACT.Identity, bias=-1.0, scale=1.0)
            nc.sync.dma_start(out=out_1[group_rows(g)].rearrange("(p t) d s -> p t d s", t=TILES)[:, t, :, :], in_=new)

        def live(g):
            return 0 <= g < GROUPS

        def stage(g, step, *args):
            if live(g):
                step(g, *args)

        done = set()
        OUT_AHEAD = 3
        CHAIN_AHEAD = 2

        def once(g, step, *args):
            if live(g) and (step, g, args) not in done:
                done.add((step, g, args))
                step(g, *args)

        def tile_stage(k, step):
            stage(k // TILES, step, k % TILES)

        def front_prepare(f):
            g, t = f // TILES, f % TILES
            if t == 0:
                once(g, new_out_tile)
            once(g, out_passes, t)

        def front_out(f):
            once(f // TILES, out_bias, f % TILES)
            front_prepare(f + 1)
            if f % TILES == TILES - 1:
                once(f // TILES, store_out)

        def begin_tile(k):
            tile_stage(k, scale_steps)
            tile_stage(k, last_inner_sum)

        def chain_first(c):
            x, phase = c // TILES + 1, c % TILES
            if phase == 0:
                once(x + 3, load_h)
                once(x - 1, share_of_both)
            if phase == 2:
                once(x, turn_tops)
            if phase == 3:
                once(x + 2, new_quantise_input)

        def chain_issue(c):
            x, phase = c // TILES + 1, c % TILES
            once(x + 1 + (phase + 1) // TILES, transpose_h_tile, (phase + 1) % TILES)
            if phase == 3 and live(x):
                load_sigmoid_table()
            if phase == 1:
                once(x, logit, 3)
                once(x, top_of)

        def chain_early(c):
            x, phase = c // TILES + 1, c % TILES
            if phase == 0:
                once(x, quantise_h)
                once(x, new_planes)
                once(x, logit, 2)
                once(x, copy_noop)
            if phase == 2:
                once(x, peak_of)
                once(x, logit, 1)
                once(x, turn_shares)
            if phase == 3:
                once(x, pop_less_peak)
                once(x, pop_less_both)

        def chain_late(c):
            x, phase = c // TILES + 1, c % TILES
            if phase == 1:
                once(x, gap_of)
                once(x, share_of_push)
                once(x, larger_share)
                once(x, log_of_larger_share)
                once(x - 1, scale_first_steps)

        def slot(k, chain):
            phase = chain[0] % TILES
            if k % TILES == 0:
                once(k // TILES + 2, load_stack)
            chain_first(chain[0])
            chain_issue(chain[0])
            if k % TILES == 0:
                once(k // TILES + 1, raise_last_row)
            chain_early(chain[0])
            if phase != 1:
                front_out(k + OUT_AHEAD)
            if phase == 0:
                once(chain[0] // TILES + 1, logit, 0)
            tile_stage(k, inner_sums)
            if phase == 1:
                front_out(k + OUT_AHEAD)
            if k < GROUPS * TILES - 1:
                feed_blend(k)
            chain_late(chain[0])
            for c in chain[1:]:
                chain_first(c)
                chain_issue(c)
                chain_early(c)
                chain_late(c)
            begin_tile(k + 1)
            for c in chain:
                if c % TILES == 2:
                    once(c // TILES + 1, first_steps)
            tile_stage(k, scale_by_q)
            tile_stage(k, add_popped_and_store)

        by_vector = nc.vector.tensor_copy

        def ahead_of_turn(step, g, *args, **how):
            done.add((step, g, args))
            step(g, *args, **how)

        once(1, load_h)
        quantise_h_by_tiles(0)
        done.add((quantise_h, 0, ()))
        for t in range(TILES):
            transpose_h_tile(0, t, "pair" if t % 2 else "quick", copier=None)
            keep_h_tile_alone(0, t)
            quantise_h_tile(0, t)
            if t == 0:
                widen_biases()
        once(2, load_h)
        once(0, load_stack)
        once(1, load_stack)
        once(3, load_h)
        turn_biases()
        keep_biases()
        once(0, new_planes)
        once(1, new_quantise_input)
        once(0, logit, 2)
        once(0, logit, 0)
        once(0, copy_noop)
        front_prepare(0)
        ahead_of_turn(transpose_h_tile, 1, 0, bank="pair", copier=None)
        ahead_of_turn(transpose_h_tile, 1, 1, bank="pair", copier=None)
        once(0, gap_of)
        once(0, peak_of)
        once(0, share_of_push)
        once(0, larger_share)
        once(0, logit, 1)
        once(0, logit, 3)
        ahead_of_turn(turn_shares, 0, copier=None)
        front_out(0)
        keep_h_tile(1, 0, by_vector)
        keep_h_tile(1, 1, by_vector)
        ahead_of_turn(transpose_h_tile, 1, 2, bank="steps", copier=None)
        ahead_of_turn(transpose_h_tile, 1, 3, bank="steps", copier=None)
        once(0, log_of_larger_share)
        once(0, pop_less_peak)
        once(0, pop_less_both)
        once(0, top_of)
        keep_shares(0, by_vector)
        front_out(1)
        once(2, new_quantise_input)
        ahead_of_turn(transpose_h_tile, 2, 0, bank="long", copier=None)
        ahead_of_turn(transpose_h_tile, 2, 1, bank="pair", copier=None)
        keep_h_tile(1, 2, by_vector)
        keep_h_tile(1, 3, by_vector)
        once(0, turn_tops)
        once(0, share_of_both)
        for t in range(2):
            keep_h_tile(2, t, nc.scalar.copy)
        once(1, quantise_h)
        feed_blend(-2)
        feed_blend(-1)
        once(0, first_steps)
        once(0, scale_first_steps)
        once(1, new_planes)
        once(1, logit, 2)
        once(1, copy_noop)
        front_out(2)
        once(1, logit, 0)
        once(4, load_h)
        once(0, raise_last_row)
        begin_tile(0)
        slot(0, (1, 2))
        for k in range(1, GROUPS * TILES):
            slot(k, (k + CHAIN_AHEAD,))
